import numpy as np
import ml_dtypes


def mxq(x, axis, fmt="e4m3"):
    dtype, down = {"e4m3": (ml_dtypes.float8_e4m3fn, 7), "e5m2": (ml_dtypes.float8_e5m2, 14)}[fmt]
    v = np.moveaxis(np.asarray(x, np.float32).astype(ml_dtypes.bfloat16).astype(np.float64), axis, -1)
    blocks = v.reshape(v.shape[:-1] + (-1, 32))
    amax = np.abs(blocks).max(-1, keepdims=True)
    byte = np.maximum(np.where(amax > 0, np.frexp(amax)[1] - 1 + 127, 0) - down, 1)
    scale = np.exp2(byte - 127.0)
    codes = (blocks / scale).astype(np.float32).astype(dtype).astype(np.float64)
    return np.moveaxis((codes * scale).reshape(v.shape), -1, axis)


WIDE = False


def mx_kscale(k):
    if not WIDE:
        return np.ones(k)
    levels = np.array([30, -30])
    if k % 512:
        return np.exp2(np.random.permutation(np.resize(levels, k // 32))).repeat(32)
    a = np.empty((k // 512, 16))
    for p in range(k // 512):
        a[p, :8] = np.random.permutation(np.resize(levels, 8))
        for g in range(8):
            far = levels[np.abs(levels - a[p, g]) >= 10]
            a[p, g + 8] = far[np.random.randint(len(far))]
    return np.exp2(a.ravel()).repeat(32)


BF16 = ml_dtypes.bfloat16


def bf(x):
    return np.asarray(x, np.float32).astype(BF16)


def f64(x):
    return np.asarray(x).astype(np.float64)


B, CIN, H, W, CP, G = 3, 2048, 16, 16, 1024, 2
CG = CP // G
HW = H * W
ATT_N = np.sqrt(HW * HW * CG / CIN + HW * CG)


def setup_inputs():
    s = mx_kscale(CIN)
    r = np.sqrt(2.5 / ATT_N) / np.sqrt(CIN)
    return {"x": bf(np.random.standard_normal((B, CIN, H, W)) * s[None, :, None, None]),
            "Wt": bf(np.random.standard_normal((CP, CIN)) / np.sqrt(CIN) / s),
            "Wp": bf(np.random.standard_normal((CP, CIN)) * r / s),
            "Wg": bf(np.random.standard_normal((CP, CIN)) * r / s)}


def reference(x, Wt, Wp, Wg):
    xq = mxq(f64(x).reshape(B, CIN, HW), 1, "e4m3")
    t = mxq(f64(Wt), 1, "e5m2") @ xq
    p = mxq(f64(Wp), 1, "e5m2") @ xq
    g = mxq(f64(Wg), 1, "e5m2") @ xq
    t = t.reshape(B, G, CG * HW)
    p = p.reshape(B, G, CG * HW)
    g = g.reshape(B, G, CG * HW)
    att = (p * g).sum(-1, keepdims=True)
    return (att * t).reshape(B, G, CG, HW)

@@ -1,0 +1,249 @@
+from contextlib import ExitStack
+
+import concourse.masks as masks
+import concourse.mybir as mybir
+
+FLOPS = 2 * 3 * 3072 * 2048 * 256
+
+F32 = mybir.dt.float32
+BF16 = mybir.dt.bfloat16
+U32 = mybir.dt.uint32
+U8 = mybir.dt.uint8
+E4 = mybir.dt.float8_e4m3fn_x4
+E5 = mybir.dt.float8_e5m2_x4
+ACT = mybir.ActivationFunctionType
+ALU = mybir.AluOpType
+AX = mybir.AxisListType
+
+P = 128
+WRAW_BUFS = 10
+
+
+def tile_spatialcgnl_pa_kernel(tc, x, Wt, Wp, Wg, out):
+    nc = tc.nc
+    units = [(Wp, 0), (Wg, 0), (Wp, 1), (Wg, 1), (Wt, 0), (Wt, 1)]
+
+    with ExitStack() as ctx:
+        const = ctx.enter_context(tc.tile_pool(name="const", bufs=1))
+        keep = ctx.enter_context(tc.tile_pool(name="keep", bufs=1))
+        wraw_pool = ctx.enter_context(tc.tile_pool(name="wrawp", bufs=WRAW_BUFS))
+        xgrp_pool = ctx.enter_context(tc.tile_pool(name="xgrpp", bufs=2))
+        grp_pool = ctx.enter_context(tc.tile_pool(name="grpp", bufs=2))
+        psb_pool = ctx.enter_context(tc.tile_pool(name="psbp", bufs=8))
+        junk_pool = ctx.enter_context(tc.tile_pool(name="junkp", bufs=2))
+        osb_pool = ctx.enter_context(tc.tile_pool(name="osbp", bufs=3))
+        psum = ctx.enter_context(tc.psum_pool(name="psum", bufs=1))
+        ctx.enter_context(tc.manual_schedule())
+
+        ident = const.tile([P, P], F32, name="ident")
+        masks.make_identity(nc, ident[:])
+        ones = const.tile([P, P], F32, name="ones")
+        nc.vector.memset(ones[:], 1.0)
+        warm = const.tile([P, 1], F32, name="warm")
+        nc.scalar.activation(out=warm[:], in_=ones[:, 0:1], func=ACT.Copy)
+        accs = const.tile([P, 12], F32, name="accs")
+        att_sb = const.tile([P, 6], F32, name="att_sb")
+
+        x_raw = {}
+        x_codes = {}
+        x_scales = {}
+        for g in range(4):
+            x_codes[g] = keep.tile([P, 768], U32, name="xc%d" % g, align_bytes=64)
+            x_scales[g] = keep.tile([P, 768], U8, name="xs%d" % g, align_bytes=64)
+        wc = {}
+        ws = {}
+        for u in range(6):
+            wc[u] = keep.tile([P, 4, 512], U32, name="wc%d" % u, align_bytes=64)
+            ws[u] = keep.tile([P, 4, 512], U8, name="ws%d" % u, align_bytes=64)
+        w_raw = {}
+        grp = {}
+        tps = {}
+        p_sb = {}
+        o_sb = {}
+        state = {"acc": 0}
+
+        def copy_on(eng, dst, src):
+            if eng == "s":
+                nc.scalar.copy(out=dst, in_=src)
+            else:
+                nc.vector.tensor_copy(out=dst, in_=src)
+
+        def load_w(t):
+            w_ap, j = units[t // 4]
+            r0 = j * 512 + (t % 4) * P
+            w_raw[t] = wraw_pool.tile([P, 2048], BF16, name="wraw%d" % t, tag="wraw")
+            nc.sync.dma_start(out=w_raw[t][:], in_=w_ap[r0 : r0 + P, :])
+
+        def load_x(b):
+            x_raw[b] = keep.tile([P, 4, 1024], BF16, name="xraw%d" % b)
+            nc.sync.dma_start(
+                out=x_raw[b][:], in_=x[b].rearrange("(g p j) h w -> p g (j h w)", g=4, p=P, j=4)
+            )
+
+        def prep_x(b):
+            xg = xgrp_pool.tile([P, 4, 1024], BF16, name="xgrp%d" % b, tag="xgrp", align_bytes=64)
+            for g in range(4):
+                copy_on(
+                    "v" if g < 2 else "s",
+                    xg[:, g, :].rearrange("p (n j) -> p n j", j=4),
+                    x_raw[b][:, g, :].rearrange("p (j n) -> p n j", j=4),
+                )
+            for g in range(4):
+                cols = slice(b * 256, (b + 1) * 256)
+                nc.vector.quantize_mx(
+                    out=x_codes[g][:, cols].bitcast(E4), scales=x_scales[g][:, cols], in_=xg[:, g, :]
+                )
+
+        def transposes(t, banks):
+            words = w_raw[t][:].bitcast(F32)
+            for h in range(2):
+                tp = psum.tile([P, 512], F32, name="tp%d_%d" % (t, h), tag="bank%d" % banks[h])
+                tps[(t, h)] = tp
+                for gl in range(2):
+                    g = 2 * h + gl
+                    for u in range(2):
+                        s = 2 * gl + u
+                        nc.tensor.transpose(
+                            tp[:, s * P : (s + 1) * P], words[:, 256 * g + u : 256 * (g + 1) : 2], ident[:]
+                        )
+
+        def evac(t, h, eng):
+            u, cb = t // 4, t % 4
+            if cb == 0 and h == 0:
+                grp[u] = grp_pool.tile([P, 4, 2048], BF16, name="grp%d" % u, tag="grp", align_bytes=64)
+            gw = grp[u][:].bitcast(F32).rearrange("p g (c u) -> p g c u", u=2)
+            copy_on(
+                eng,
+                gw[:, 2 * h : 2 * h + 2, cb * P : (cb + 1) * P, :],
+                tps[(t, h)][:].rearrange("p (g u c) -> p g c u", g=2, u=2),
+            )
+
+        def quant_w(u):
+            for g in range(4):
+                nc.vector.quantize_mx(
+                    out=wc[u][:, g, :].bitcast(E5), scales=ws[u][:, g, :], in_=grp[u][:, g, :]
+                )
+
+        def next_acc(name):
+            bank = 2 + state["acc"] % 4
+            state["acc"] = state["acc"] + 1
+            return psum.tile([P, 512], F32, name=name, tag="bank%d" % bank)
+
+        def group_b(u, m):
+            acc = next_acc("acc%d_%d" % (u, m))
+            cols = slice(m * P, (m + 1) * P)
+            for g in range(4):
+                nc.tensor.matmul_mx(
+                    out=acc[:],
+                    lhsT=x_codes[g][:, cols].bitcast(E4),
+                    lhsT_scale=x_scales[g][:, cols],
+                    rhs=wc[u][:, g, :].bitcast(E5),
+                    rhs_scale=ws[u][:, g, :],
+                    start=(g == 0),
+                    stop=(g == 3),
+                )
+            j = units[u][1]
+            if u % 2 == 0:
+                p_sb[(j, m)] = psb_pool.tile([P, 512], F32, name="psb%d_%d" % (j, m), tag="psb")
+                nc.scalar.copy(out=p_sb[(j, m)][:], in_=acc[:])
+            else:
+                junk = junk_pool.tile([P, 512], F32, name="junk%d_%d" % (j, m), tag="junk")
+                nc.vector.scalar_tensor_tensor(
+                    out=junk[:],
+                    in0=acc[:],
+                    scalar=1.0,
+                    in1=p_sb[(j, m)][:],
+                    op0=ALU.mult,
+                    op1=ALU.mult,
+                    accum_out=accs[:, 6 * j + m : 6 * j + m + 1],
+                )
+
+        def attention(j):
+            att_ps = next_acc("attps%d" % j)
+            nc.tensor.matmul(
+                out=att_ps[:, 0:6], lhsT=ones[:], rhs=accs[:, 6 * j : 6 * j + 6], start=True, stop=True
+            )
+            nc.vector.tensor_reduce(
+                out=att_sb[:, 3 * j : 3 * j + 3],
+                in_=att_ps[:, 0:6].rearrange("p (b h) -> p b h", h=2),
+                axis=AX.X,
+                op=ALU.add,
+            )
+
+        def group_t(u, cb, pair):
+            j = units[u][1]
+            acc = next_acc("acct%d_%d_%d" % (u, cb, pair))
+            ch = slice(cb * P, (cb + 1) * P)
+            cols = slice(pair * 256, pair * 256 + 512)
+            for g in range(4):
+                nc.tensor.matmul_mx(
+                    out=acc[:],
+                    lhsT=wc[u][:, g, ch].bitcast(E5),
+                    lhsT_scale=ws[u][:, g, ch],
+                    rhs=x_codes[g][:, cols].bitcast(E4),
+                    rhs_scale=x_scales[g][:, cols],
+                    start=(g == 0),
+                    stop=(g == 3),
+                )
+            if pair == 0:
+                o_sb[(u, cb)] = osb_pool.tile([P, 3, 256], F32, name="osb%d_%d" % (u, cb), tag="osb")
+                for b in range(2):
+                    nc.scalar.activation(
+                        out=o_sb[(u, cb)][:, b, :],
+                        in_=acc[:, b * 256 : (b + 1) * 256],
+                        func=ACT.Copy,
+                        scale=att_sb[:, 3 * j + b : 3 * j + b + 1],
+                    )
+            else:
+                nc.vector.tensor_scalar(
+                    out=o_sb[(u, cb)][:, 2, :],
+                    in0=acc[:, 256:512],
+                    scalar1=att_sb[:, 3 * j + 2 : 3 * j + 3],
+                    scalar2=None,
+                    op0=ALU.mult,
+                )
+                nc.sync.dma_start(
+                    out=out[:, j, cb * P : (cb + 1) * P, :].rearrange("b c n -> c b n"), in_=o_sb[(u, cb)][:]
+                )
+
+        def block(k):
+            u, h = k // 2, k % 2
+            if u < 4:
+                for m in range(3 * h, 3 * h + 3):
+                    group_b(u, m)
+            else:
+                for cb in range(2 * h, 2 * h + 2):
+                    for pair in range(2):
+                        group_t(u, cb, pair)
+
+        for t in range(4):
+            load_w(t)
+        load_x(0)
+        load_w(4)
+        load_w(5)
+        load_x(1)
+        load_x(2)
+        for t in range(6, WRAW_BUFS):
+            load_w(t)
+
+        for r in range(14):
+            if r < 12:
+                for t, banks in ((2 * r, (6, 7)), (2 * r + 1, (0, 1))):
+                    transposes(t, banks)
+                    evac(t, 0, "s")
+                    evac(t, 1, "s" if r >= 4 else "v")
+                    if t + WRAW_BUFS < 24:
+                        load_w(t + WRAW_BUFS)
+                if r % 2 == 1:
+                    quant_w(r // 2)
+            if r == 1:
+                prep_x(0)
+            if r == 2:
+                prep_x(1)
+                prep_x(2)
+            if r >= 2:
+                block(r - 2)
+            if r == 6:
+                attention(0)
+            if r == 10:
+                attention(1)

@@ -16,22 +16,84 @@ ALU = mybir.AluOpType
 AX = mybir.AxisListType
 
 P = 128
-WRAW_BUFS = 10
+
+CFG = {
+    "NB": 8, "PRE": 8, "pc_eng": ("V", "V"),
+    "loads": ["w0", "w1", "w2", "w3", "x0", "w4", "w5", "x1", "x2"],
+    "ix": ["V", "V", "S", "S"], "ep": ["S", "S"], "et": ["S", "V", "S", "V"],
+    "ev_head": ("S", "V"), "ev": ("S", "S"), "EVH": 8, "qc": (0,), "xprep": {1: (0,), 2: (1, 2)},
+}
+
+
+def make_plan(cfg):
+    NB = cfg['NB']; PRE = cfg['PRE']; plan = []; A = plan.append
+    st = {'acc': 0}
+    def nb():
+        b = 2 + st['acc'] % 4; st['acc'] += 1; return b
+    def pre(t):
+        return cfg['pc_eng'][(t // 4) % 2] if t >= PRE else None
+    nw = 0
+    for o in cfg['loads']:
+        if o[0] == 'w':
+            A(('LW', int(o[1:]))); nw += 1
+        else:
+            for g in range(4): A(('LX', int(o[1:]), g))
+    for t in range(nw, NB): A(('LW', t))
+    def prep_x(b):
+        for g in range(4): A(('IX', b, g, cfg['ix'][g]))
+        for g in range(4): A(('QX', b, g))
+    def back(u):
+        for half in range(2):
+            bank = nb()
+            A(('BT', u, half, bank)); A(('EB', u, half, 'V', bank))
+    def block(k):
+        u, h = k // 2, k % 2
+        if u < 4:
+            for m in range(3*h, 3*h+3):
+                A(('GB', u, m, cfg['ep'][m % 2] if u % 2 == 0 else 'V', nb()))
+        elif h == 0:
+            A(('GB', u, 4, 'S', nb())); A(('GB', u, 5, 'V', nb())); A(('GA', u, 0, cfg['et'][0], nb()))
+        else:
+            for cb in (1,2,3): A(('GA', u, cb, cfg['et'][cb], nb()))
+    for r in range(14):
+        if r == 7: A(('ATT', 0, nb()))
+        if r == 11: A(('ATT', 1, nb()))
+        if r < 12:
+            for t, banks in ((2*r, (6,7)), (2*r+1, (0,1))):
+                A(('T', t, banks[0], banks[1], pre(t) is not None))
+                ev = cfg['ev_head'] if t < cfg['EVH'] else cfg['ev']
+                A(('EV', t, 0, ev[0], banks[0])); A(('EV', t, 1, ev[1], banks[1]))
+                if t + NB < 24: A(('LW', t + NB))
+                if t // 4 in cfg['qc']:
+                    for g in range(4): A(('QC', t, g))
+            if r == 11: back(4)
+            for t in (2*r+2, 2*r+3):
+                if t < 24 and pre(t): A(('PC', t, pre(t)))
+            if r % 2 == 1 and (r//2) not in cfg['qc']:
+                for g in range(4): A(('QU', r//2, g))
+        for b in cfg['xprep'].get(r, ()): prep_x(b)
+        if r >= 2: block(r - 2)
+        if r == 12: back(5)
+    return plan
 
 
 def tile_spatialcgnl_pa_kernel(tc, x, Wt, Wp, Wg, out):
     nc = tc.nc
     units = [(Wp, 0), (Wg, 0), (Wp, 1), (Wg, 1), (Wt, 0), (Wt, 1)]
+    plan = make_plan(CFG)
 
     with ExitStack() as ctx:
         const = ctx.enter_context(tc.tile_pool(name="const", bufs=1))
         keep = ctx.enter_context(tc.tile_pool(name="keep", bufs=1))
-        wraw_pool = ctx.enter_context(tc.tile_pool(name="wrawp", bufs=WRAW_BUFS))
-        xgrp_pool = ctx.enter_context(tc.tile_pool(name="xgrpp", bufs=2))
+        wraw_pool = ctx.enter_context(tc.tile_pool(name="wrawp", bufs=CFG["NB"]))
+        wde_pool = ctx.enter_context(tc.tile_pool(name="wdep", bufs=4))
+        xgrp_pool = ctx.enter_context(tc.tile_pool(name="xgrpp", bufs=4))
         grp_pool = ctx.enter_context(tc.tile_pool(name="grpp", bufs=2))
         psb_pool = ctx.enter_context(tc.tile_pool(name="psbp", bufs=8))
-        junk_pool = ctx.enter_context(tc.tile_pool(name="junkp", bufs=2))
-        osb_pool = ctx.enter_context(tc.tile_pool(name="osbp", bufs=3))
+        junk_pool = ctx.enter_context(tc.tile_pool(name="junkp", bufs=1))
+        tt_pool = ctx.enter_context(tc.tile_pool(name="ttp", bufs=4))
+        o01_pool = ctx.enter_context(tc.tile_pool(name="o01p", bufs=3))
+        o2_pool = ctx.enter_context(tc.tile_pool(name="o2p", bufs=2))
         psum = ctx.enter_context(tc.psum_pool(name="psum", bufs=1))
         ctx.enter_context(tc.manual_schedule())
 
@@ -44,7 +106,6 @@ def tile_spatialcgnl_pa_kernel(tc, x, Wt, Wp, Wg, out):
         accs = const.tile([P, 12], F32, name="accs")
         att_sb = const.tile([P, 6], F32, name="att_sb")
 
-        x_raw = {}
         x_codes = {}
         x_scales = {}
         for g in range(4):
@@ -55,59 +116,83 @@ def tile_spatialcgnl_pa_kernel(tc, x, Wt, Wp, Wg, out):
         for u in range(6):
             wc[u] = keep.tile([P, 4, 512], U32, name="wc%d" % u, align_bytes=64)
             ws[u] = keep.tile([P, 4, 512], U8, name="ws%d" % u, align_bytes=64)
+        x_raw = {}
+        x_grp = {}
         w_raw = {}
+        w_de = {}
         grp = {}
         tps = {}
         p_sb = {}
-        o_sb = {}
-        state = {"acc": 0}
+        t_sb = {}
+
+        def bank_tile(name, bank):
+            return psum.tile([P, 512], F32, name=name, tag="bank%d" % bank)
 
         def copy_on(eng, dst, src):
-            if eng == "s":
+            if eng == "S":
                 nc.scalar.copy(out=dst, in_=src)
             else:
                 nc.vector.tensor_copy(out=dst, in_=src)
 
-        def load_w(t):
+        def scale_on(eng, dst, src, col):
+            if eng == "S":
+                nc.scalar.activation(out=dst, in_=src, func=ACT.Copy, scale=att_sb[:, col : col + 1])
+            else:
+                nc.vector.tensor_scalar(
+                    out=dst, in0=src, scalar1=att_sb[:, col : col + 1], scalar2=None, op0=ALU.mult
+                )
+
+        def op_lw(t):
             w_ap, j = units[t // 4]
             r0 = j * 512 + (t % 4) * P
             w_raw[t] = wraw_pool.tile([P, 2048], BF16, name="wraw%d" % t, tag="wraw")
             nc.sync.dma_start(out=w_raw[t][:], in_=w_ap[r0 : r0 + P, :])
 
-        def load_x(b):
-            x_raw[b] = keep.tile([P, 4, 1024], BF16, name="xraw%d" % b)
+        def op_lx(b, g):
+            x_raw[(b, g)] = keep.tile([P, 1024], BF16, name="xraw%d_%d" % (b, g))
             nc.sync.dma_start(
-                out=x_raw[b][:], in_=x[b].rearrange("(g p j) h w -> p g (j h w)", g=4, p=P, j=4)
+                out=x_raw[(b, g)][:],
+                in_=x[b, g * 512 : (g + 1) * 512].rearrange("(p j) h w -> p (j h w)", j=4),
             )
 
-        def prep_x(b):
-            xg = xgrp_pool.tile([P, 4, 1024], BF16, name="xgrp%d" % b, tag="xgrp", align_bytes=64)
-            for g in range(4):
-                copy_on(
-                    "v" if g < 2 else "s",
-                    xg[:, g, :].rearrange("p (n j) -> p n j", j=4),
-                    x_raw[b][:, g, :].rearrange("p (j n) -> p n j", j=4),
-                )
-            for g in range(4):
-                cols = slice(b * 256, (b + 1) * 256)
-                nc.vector.quantize_mx(
-                    out=x_codes[g][:, cols].bitcast(E4), scales=x_scales[g][:, cols], in_=xg[:, g, :]
-                )
+        def op_ix(b, g, eng):
+            x_grp[(b, g)] = xgrp_pool.tile([P, 1024], BF16, name="xgrp%d_%d" % (b, g), tag="xgrp", align_bytes=64)
+            copy_on(
+                eng,
+                x_grp[(b, g)][:].rearrange("p (n j) -> p n j", j=4),
+                x_raw[(b, g)][:].rearrange("p (j n) -> p n j", j=4),
+            )
 
-        def transposes(t, banks):
+        def op_qx(b, g):
+            cols = slice(b * 256, (b + 1) * 256)
+            nc.vector.quantize_mx(
+                out=x_codes[g][:, cols].bitcast(E4), scales=x_scales[g][:, cols], in_=x_grp[(b, g)][:]
+            )
+
+        def op_pc(t, eng):
+            w_de[t] = wde_pool.tile([P, 1024], F32, name="wde%d" % t, tag="wde")
+            copy_on(
+                eng,
+                w_de[t][:].rearrange("c (g u p) -> c g u p", g=4, u=2),
+                w_raw[t][:].bitcast(F32).rearrange("c (g p u) -> c g u p", g=4, u=2),
+            )
+
+        def op_t(t, bank0, bank1, pre):
             words = w_raw[t][:].bitcast(F32)
-            for h in range(2):
-                tp = psum.tile([P, 512], F32, name="tp%d_%d" % (t, h), tag="bank%d" % banks[h])
+            for h, bank in ((0, bank0), (1, bank1)):
+                tp = bank_tile("tp%d_%d" % (t, h), bank)
                 tps[(t, h)] = tp
                 for gl in range(2):
                     g = 2 * h + gl
                     for u in range(2):
                         s = 2 * gl + u
-                        nc.tensor.transpose(
-                            tp[:, s * P : (s + 1) * P], words[:, 256 * g + u : 256 * (g + 1) : 2], ident[:]
-                        )
+                        if pre:
+                            src = w_de[t][:, (2 * g + u) * P : (2 * g + u + 1) * P]
+                        else:
+                            src = words[:, 256 * g + u : 256 * (g + 1) : 2]
+                        nc.tensor.transpose(tp[:, s * P : (s + 1) * P], src, ident[:])
 
-        def evac(t, h, eng):
+        def op_ev(t, h, eng, bank):
             u, cb = t // 4, t % 4
             if cb == 0 and h == 0:
                 grp[u] = grp_pool.tile([P, 4, 2048], BF16, name="grp%d" % u, tag="grp", align_bytes=64)
@@ -118,19 +203,20 @@ def tile_spatialcgnl_pa_kernel(tc, x, Wt, Wp, Wg, out):
                 tps[(t, h)][:].rearrange("p (g u c) -> p g c u", g=2, u=2),
             )
 
-        def quant_w(u):
-            for g in range(4):
-                nc.vector.quantize_mx(
-                    out=wc[u][:, g, :].bitcast(E5), scales=ws[u][:, g, :], in_=grp[u][:, g, :]
-                )
+        def op_qu(u, g):
+            nc.vector.quantize_mx(out=wc[u][:, g, :].bitcast(E5), scales=ws[u][:, g, :], in_=grp[u][:, g, :])
 
-        def next_acc(name):
-            bank = 2 + state["acc"] % 4
-            state["acc"] = state["acc"] + 1
-            return psum.tile([P, 512], F32, name=name, tag="bank%d" % bank)
+        def op_qc(t, g):
+            u, cb = t // 4, t % 4
+            ch = slice(cb * P, (cb + 1) * P)
+            nc.vector.quantize_mx(
+                out=wc[u][:, g, ch].bitcast(E5),
+                scales=ws[u][:, g, ch],
+                in_=grp[u][:, g, cb * 512 : (cb + 1) * 512],
+            )
 
-        def group_b(u, m):
-            acc = next_acc("acc%d_%d" % (u, m))
+        def op_gb(u, m, eng, bank):
+            acc = bank_tile("acc%d_%d" % (u, m), bank)
             cols = slice(m * P, (m + 1) * P)
             for g in range(4):
                 nc.tensor.matmul_mx(
@@ -143,9 +229,12 @@ def tile_spatialcgnl_pa_kernel(tc, x, Wt, Wp, Wg, out):
                     stop=(g == 3),
                 )
             j = units[u][1]
-            if u % 2 == 0:
+            if u >= 4:
+                t_sb[(u, m)] = tt_pool.tile([P, 512], F32, name="tsb%d_%d" % (u, m), tag="tsb")
+                scale_on(eng, t_sb[(u, m)][:], acc[:], 3 * j + 2)
+            elif u % 2 == 0:
                 p_sb[(j, m)] = psb_pool.tile([P, 512], F32, name="psb%d_%d" % (j, m), tag="psb")
-                nc.scalar.copy(out=p_sb[(j, m)][:], in_=acc[:])
+                copy_on(eng, p_sb[(j, m)][:], acc[:])
             else:
                 junk = junk_pool.tile([P, 512], F32, name="junk%d_%d" % (j, m), tag="junk")
                 nc.vector.scalar_tensor_tensor(
@@ -158,8 +247,8 @@ def tile_spatialcgnl_pa_kernel(tc, x, Wt, Wp, Wg, out):
                     accum_out=accs[:, 6 * j + m : 6 * j + m + 1],
                 )
 
-        def attention(j):
-            att_ps = next_acc("attps%d" % j)
+        def op_att(j, bank):
+            att_ps = bank_tile("attps%d" % j, bank)
             nc.tensor.matmul(
                 out=att_ps[:, 0:6], lhsT=ones[:], rhs=accs[:, 6 * j : 6 * j + 6], start=True, stop=True
             )
@@ -170,80 +259,47 @@ def tile_spatialcgnl_pa_kernel(tc, x, Wt, Wp, Wg, out):
                 op=ALU.add,
             )
 
-        def group_t(u, cb, pair):
+        def op_ga(u, cb, eng, bank):
             j = units[u][1]
-            acc = next_acc("acct%d_%d_%d" % (u, cb, pair))
+            acc = bank_tile("acct%d_%d" % (u, cb), bank)
             ch = slice(cb * P, (cb + 1) * P)
-            cols = slice(pair * 256, pair * 256 + 512)
             for g in range(4):
                 nc.tensor.matmul_mx(
                     out=acc[:],
                     lhsT=wc[u][:, g, ch].bitcast(E5),
                     lhsT_scale=ws[u][:, g, ch],
-                    rhs=x_codes[g][:, cols].bitcast(E4),
-                    rhs_scale=x_scales[g][:, cols],
+                    rhs=x_codes[g][:, 0:512].bitcast(E4),
+                    rhs_scale=x_scales[g][:, 0:512],
                     start=(g == 0),
                     stop=(g == 3),
                 )
-            if pair == 0:
-                o_sb[(u, cb)] = osb_pool.tile([P, 3, 256], F32, name="osb%d_%d" % (u, cb), tag="osb")
-                for b in range(2):
-                    nc.scalar.activation(
-                        out=o_sb[(u, cb)][:, b, :],
-                        in_=acc[:, b * 256 : (b + 1) * 256],
-                        func=ACT.Copy,
-                        scale=att_sb[:, 3 * j + b : 3 * j + b + 1],
+            o01 = o01_pool.tile([P, 2, 256], F32, name="o01_%d_%d" % (u, cb), tag="o01")
+            for b in range(2):
+                scale_on(eng, o01[:, b, :], acc[:, b * 256 : (b + 1) * 256], 3 * j + b)
+            nc.sync.dma_start(out=out[0:2, j, ch, :].rearrange("b c n -> c b n"), in_=o01[:])
+
+        def op_bt(u, half, bank):
+            tp = bank_tile("bt%d_%d" % (u, half), bank)
+            tps[("bt", u, half)] = tp
+            for l in range(2):
+                cb = 2 * half + l
+                for mh in range(2):
+                    s = 2 * l + mh
+                    nc.tensor.transpose(
+                        tp[:, s * P : (s + 1) * P], t_sb[(u, 4 + mh)][:, cb * P : (cb + 1) * P], ident[:]
                     )
-            else:
-                nc.vector.tensor_scalar(
-                    out=o_sb[(u, cb)][:, 2, :],
-                    in0=acc[:, 256:512],
-                    scalar1=att_sb[:, 3 * j + 2 : 3 * j + 3],
-                    scalar2=None,
-                    op0=ALU.mult,
-                )
-                nc.sync.dma_start(
-                    out=out[:, j, cb * P : (cb + 1) * P, :].rearrange("b c n -> c b n"), in_=o_sb[(u, cb)][:]
-                )
 
-        def block(k):
-            u, h = k // 2, k % 2
-            if u < 4:
-                for m in range(3 * h, 3 * h + 3):
-                    group_b(u, m)
-            else:
-                for cb in range(2 * h, 2 * h + 2):
-                    for pair in range(2):
-                        group_t(u, cb, pair)
+        def op_eb(u, half, eng, bank):
+            j = units[u][1]
+            o2 = o2_pool.tile([P, 2, 256], F32, name="o2_%d_%d" % (u, half), tag="o2")
+            copy_on(eng, o2[:].rearrange("c l n -> c (l n)"), tps[("bt", u, half)][:])
+            nc.sync.dma_start(
+                out=out[2, j, half * 256 : (half + 1) * 256, :].rearrange("(l c) n -> c l n", l=2), in_=o2[:]
+            )
 
-        for t in range(4):
-            load_w(t)
-        load_x(0)
-        load_w(4)
-        load_w(5)
-        load_x(1)
-        load_x(2)
-        for t in range(6, WRAW_BUFS):
-            load_w(t)
-
-        for r in range(14):
-            if r < 12:
-                for t, banks in ((2 * r, (6, 7)), (2 * r + 1, (0, 1))):
-                    transposes(t, banks)
-                    evac(t, 0, "s")
-                    evac(t, 1, "s" if r >= 4 else "v")
-                    if t + WRAW_BUFS < 24:
-                        load_w(t + WRAW_BUFS)
-                if r % 2 == 1:
-                    quant_w(r // 2)
-            if r == 1:
-                prep_x(0)
-            if r == 2:
-                prep_x(1)
-                prep_x(2)
-            if r >= 2:
-                block(r - 2)
-            if r == 6:
-                attention(0)
-            if r == 10:
-                attention(1)
+        table = {
+            "LW": op_lw, "LX": op_lx, "IX": op_ix, "QX": op_qx, "PC": op_pc, "T": op_t, "EV": op_ev,
+            "QU": op_qu, "QC": op_qc, "GB": op_gb, "ATT": op_att, "GA": op_ga, "BT": op_bt, "EB": op_eb,
+        }
+        for step in plan:
+            table[step[0]](*step[1:])

@@ -21,7 +21,10 @@ CFG = {
     "NB": 8, "PRE": 8, "pc_eng": ("V", "V"),
     "loads": ["w0", "w1", "w2", "w3", "x0", "w4", "w5", "x1", "x2"],
     "ix": ["V", "V", "S", "S"], "ep": ["S", "S"], "et": ["S", "V", "S", "V"],
-    "ev_head": ("S", "V"), "ev": ("S", "S"), "EVH": 8, "qc": (0,), "xprep": {1: (0,), 2: (1, 2)},
+    "ev_head": ("S", "V"), "ev": ("S", "S"), "EVH": 8, "qc": (0,), "O01": 5, "DT": 6, "DPT": 2,
+    "seq": ["D6", "T0", "T1", "D2", "X0", "T2", "X1", "X2", "B0", "T3", "B1", "T4", "B2",
+            "T5", "B3", "T6", "B4", "A0", "T7", "B5", "T8", "B6", "T9", "B7", "T10", "B8", "A1", "T11", "B9",
+            "B10", "K5", "B11"],
 }
 
 
@@ -55,25 +58,32 @@ def make_plan(cfg):
             A(('GB', u, 4, 'S', nb())); A(('GB', u, 5, 'V', nb())); A(('GA', u, 0, cfg['et'][0], nb()))
         else:
             for cb in (1,2,3): A(('GA', u, cb, cfg['et'][cb], nb()))
-    for r in range(14):
-        if r == 7: A(('ATT', 0, nb()))
-        if r == 11: A(('ATT', 1, nb()))
-        if r < 12:
-            for t, banks in ((2*r, (6,7)), (2*r+1, (0,1))):
-                A(('T', t, banks[0], banks[1], pre(t) is not None))
-                ev = cfg['ev_head'] if t < cfg['EVH'] else cfg['ev']
-                A(('EV', t, 0, ev[0], banks[0])); A(('EV', t, 1, ev[1], banks[1]))
-                if t + NB < 24: A(('LW', t + NB))
-                if t // 4 in cfg['qc']:
-                    for g in range(4): A(('QC', t, g))
-            if r == 11: back(4)
-            for t in (2*r+2, 2*r+3):
-                if t < 24 and pre(t): A(('PC', t, pre(t)))
-            if r % 2 == 1 and (r//2) not in cfg['qc']:
-                for g in range(4): A(('QU', r//2, g))
-        for b in cfg['xprep'].get(r, ()): prep_x(b)
-        if r >= 2: block(r - 2)
-        if r == 12: back(5)
+    def tile_t(t):
+        banks = (6, 7) if t % 2 == 0 else (0, 1)
+        A(('T', t, banks[0], banks[1], pre(t) is not None))
+        if t < cfg['DT']: A(('D', cfg['DPT']))
+        ev = cfg['ev_head'] if t < cfg['EVH'] else cfg['ev']
+        A(('EV', t, 0, ev[0], banks[0])); A(('EV', t, 1, ev[1], banks[1]))
+        if t + NB < 24: A(('LW', t + NB))
+        if t // 4 in cfg['qc']:
+            for g in range(4): A(('QC', t, g))
+    def trun(r):
+        tile_t(2*r); tile_t(2*r+1)
+        if r == 11: back(4)
+        for t in (2*r+2, 2*r+3):
+            if t < 24 and pre(t) and t >= cfg.get('AUTOPC', 0): A(('PC', t, pre(t)))
+        if r % 2 == 1 and (r//2) not in cfg['qc']:
+            for g in range(4): A(('QU', r//2, g))
+    for item in cfg['seq']:
+        kind, n = item[0], int(item[1:])
+        if kind == 'T': trun(n)
+        elif kind == 'B': block(n)
+        elif kind == 'X': prep_x(n)
+        elif kind == 'K': back(n)
+        elif kind == 'P': A(('PC', n, pre(n)))
+        elif kind == 'D': A(('D', n))
+        elif kind == 'G': A(('GB', 0, n, cfg['ep'][n % 2], (2, 3, 4, 5, 6, 7)[n]))
+        else: A(('ATT', n, nb()))
     return plan
 
 
@@ -92,11 +102,13 @@ def tile_spatialcgnl_pa_kernel(tc, x, Wt, Wp, Wg, out):
         psb_pool = ctx.enter_context(tc.tile_pool(name="psbp", bufs=8))
         junk_pool = ctx.enter_context(tc.tile_pool(name="junkp", bufs=1))
         tt_pool = ctx.enter_context(tc.tile_pool(name="ttp", bufs=4))
-        o01_pool = ctx.enter_context(tc.tile_pool(name="o01p", bufs=3))
+        o01_pool = ctx.enter_context(tc.tile_pool(name="o01p", bufs=CFG["O01"]))
         o2_pool = ctx.enter_context(tc.tile_pool(name="o2p", bufs=2))
         psum = ctx.enter_context(tc.psum_pool(name="psum", bufs=1))
         ctx.enter_context(tc.manual_schedule())
 
+        dz = const.tile([P, 512], BF16, name="dz")
+        nc.vector.memset(dz[:], 0.0)
         ident = const.tile([P, P], F32, name="ident")
         masks.make_identity(nc, ident[:])
         ones = const.tile([P, P], F32, name="ones")
@@ -124,6 +136,7 @@ def tile_spatialcgnl_pa_kernel(tc, x, Wt, Wp, Wg, out):
         tps = {}
         p_sb = {}
         t_sb = {}
+        state = {"d": 0}
 
         def bank_tile(name, bank):
             return psum.tile([P, 512], F32, name=name, tag="bank%d" % bank)
@@ -141,6 +154,12 @@ def tile_spatialcgnl_pa_kernel(tc, x, Wt, Wp, Wg, out):
                 nc.vector.tensor_scalar(
                     out=dst, in0=src, scalar1=att_sb[:, col : col + 1], scalar2=None, op0=ALU.mult
                 )
+
+        def op_d(n):
+            state["d"] = state["d"] + 1
+            dps = bank_tile("dummy%d" % state["d"], 5)
+            for i in range(n):
+                nc.tensor.matmul(out=dps[:], lhsT=dz[:, 0:P], rhs=dz[:], start=True, stop=True)
 
         def op_lw(t):
             w_ap, j = units[t // 4]
@@ -299,7 +318,7 @@ def tile_spatialcgnl_pa_kernel(tc, x, Wt, Wp, Wg, out):
 
         table = {
             "LW": op_lw, "LX": op_lx, "IX": op_ix, "QX": op_qx, "PC": op_pc, "T": op_t, "EV": op_ev,
-            "QU": op_qu, "QC": op_qc, "GB": op_gb, "ATT": op_att, "GA": op_ga, "BT": op_bt, "EB": op_eb,
+            "QU": op_qu, "D": op_d, "QC": op_qc, "GB": op_gb, "ATT": op_att, "GA": op_ga, "BT": op_bt, "EB": op_eb,
         }
         for step in plan:
             table[step[0]](*step[1:])

@@ -9,316 +9,334 @@ F32 = mybir.dt.float32
 BF16 = mybir.dt.bfloat16
 U32 = mybir.dt.uint32
 U8 = mybir.dt.uint8
-E4 = mybir.dt.float8_e4m3fn_x4
-E5 = mybir.dt.float8_e5m2_x4
-ACT = mybir.ActivationFunctionType
-ALU = mybir.AluOpType
-AX = mybir.AxisListType
+E4M3_X4 = mybir.dt.float8_e4m3fn_x4
+E5M2_X4 = mybir.dt.float8_e5m2_x4
+COPY = mybir.ActivationFunctionType.Copy
+MULT = mybir.AluOpType.mult
+ADD = mybir.AluOpType.add
 
 P = 128
-
-CFG = {
-    "NB": 8, "PRE": 8, "pc_eng": ("V", "V"),
-    "loads": ["w0", "w1", "w2", "w3", "x0", "w4", "w5", "x1", "x2"],
-    "ix": ["V", "V", "S", "S"], "ep": ["S", "S"], "et": ["S", "V", "S", "V"],
-    "ev_head": ("S", "V"), "ev": ("S", "S"), "EVH": 8, "qc": (0,), "O01": 5, "DT": 6, "DPT": 2,
-    "seq": ["D6", "T0", "T1", "D2", "X0", "T2", "X1", "X2", "B0", "T3", "B1", "T4", "B2",
-            "T5", "B3", "T6", "B4", "A0", "T7", "B5", "T8", "B6", "T9", "B7", "T10", "B8", "A1", "T11", "B9",
-            "B10", "K5", "B11"],
-}
-
-
-def make_plan(cfg):
-    NB = cfg['NB']; PRE = cfg['PRE']; plan = []; A = plan.append
-    st = {'acc': 0}
-    def nb():
-        b = 2 + st['acc'] % 4; st['acc'] += 1; return b
-    def pre(t):
-        return cfg['pc_eng'][(t // 4) % 2] if t >= PRE else None
-    nw = 0
-    for o in cfg['loads']:
-        if o[0] == 'w':
-            A(('LW', int(o[1:]))); nw += 1
-        else:
-            for g in range(4): A(('LX', int(o[1:]), g))
-    for t in range(nw, NB): A(('LW', t))
-    def prep_x(b):
-        for g in range(4): A(('IX', b, g, cfg['ix'][g]))
-        for g in range(4): A(('QX', b, g))
-    def back(u):
-        for half in range(2):
-            bank = nb()
-            A(('BT', u, half, bank)); A(('EB', u, half, 'V', bank))
-    def block(k):
-        u, h = k // 2, k % 2
-        if u < 4:
-            for m in range(3*h, 3*h+3):
-                A(('GB', u, m, cfg['ep'][m % 2] if u % 2 == 0 else 'V', nb()))
-        elif h == 0:
-            A(('GB', u, 4, 'S', nb())); A(('GB', u, 5, 'V', nb())); A(('GA', u, 0, cfg['et'][0], nb()))
-        else:
-            for cb in (1,2,3): A(('GA', u, cb, cfg['et'][cb], nb()))
-    def tile_t(t):
-        banks = (6, 7) if t % 2 == 0 else (0, 1)
-        A(('T', t, banks[0], banks[1], pre(t) is not None))
-        if t < cfg['DT']: A(('D', cfg['DPT']))
-        ev = cfg['ev_head'] if t < cfg['EVH'] else cfg['ev']
-        A(('EV', t, 0, ev[0], banks[0])); A(('EV', t, 1, ev[1], banks[1]))
-        if t + NB < 24: A(('LW', t + NB))
-        if t // 4 in cfg['qc']:
-            for g in range(4): A(('QC', t, g))
-    def trun(r):
-        tile_t(2*r); tile_t(2*r+1)
-        if r == 11: back(4)
-        for t in (2*r+2, 2*r+3):
-            if t < 24 and pre(t) and t >= cfg.get('AUTOPC', 0): A(('PC', t, pre(t)))
-        if r % 2 == 1 and (r//2) not in cfg['qc']:
-            for g in range(4): A(('QU', r//2, g))
-    for item in cfg['seq']:
-        kind, n = item[0], int(item[1:])
-        if kind == 'T': trun(n)
-        elif kind == 'B': block(n)
-        elif kind == 'X': prep_x(n)
-        elif kind == 'K': back(n)
-        elif kind == 'P': A(('PC', n, pre(n)))
-        elif kind == 'D': A(('D', n))
-        elif kind == 'G': A(('GB', 0, n, cfg['ep'][n % 2], (2, 3, 4, 5, 6, 7)[n]))
-        else: A(('ATT', n, nb()))
-    return plan
+PASSES = 4
+STRIPS = 24
+ROUNDS = STRIPS // 2
+RAW_BUFS = 8
+FIRST_REORDERED = 8
+STRIPWISE_QUANTISED = 8
+TRANSPOSE_BANKS = ((6, 7), (0, 1))
+FIRST_SUM_BANK = 2
+SUM_BANKS = 4
+X_COPIES_ON_VECTOR = (3, 3, 2)
+FIRST_REGULAR_ROUND = 6
+BLOCK_LAG = 2
+ATT_ROUND = {7: 0, 11: 1}
+T_UNITS = (4, 5)
 
 
 def tile_spatialcgnl_pa_kernel(tc, x, Wt, Wp, Wg, out):
     nc = tc.nc
     units = [(Wp, 0), (Wg, 0), (Wp, 1), (Wg, 1), (Wt, 0), (Wt, 1)]
-    plan = make_plan(CFG)
 
     with ExitStack() as ctx:
         const = ctx.enter_context(tc.tile_pool(name="const", bufs=1))
         keep = ctx.enter_context(tc.tile_pool(name="keep", bufs=1))
-        wraw_pool = ctx.enter_context(tc.tile_pool(name="wrawp", bufs=CFG["NB"]))
-        wde_pool = ctx.enter_context(tc.tile_pool(name="wdep", bufs=4))
-        xgrp_pool = ctx.enter_context(tc.tile_pool(name="xgrpp", bufs=4))
-        grp_pool = ctx.enter_context(tc.tile_pool(name="grpp", bufs=2))
-        psb_pool = ctx.enter_context(tc.tile_pool(name="psbp", bufs=8))
-        junk_pool = ctx.enter_context(tc.tile_pool(name="junkp", bufs=1))
-        tt_pool = ctx.enter_context(tc.tile_pool(name="ttp", bufs=4))
-        o01_pool = ctx.enter_context(tc.tile_pool(name="o01p", bufs=CFG["O01"]))
-        o2_pool = ctx.enter_context(tc.tile_pool(name="o2p", bufs=2))
+        raw_pool = ctx.enter_context(tc.tile_pool(name="raw", bufs=RAW_BUFS))
+        reordered_pool = ctx.enter_context(tc.tile_pool(name="reordered", bufs=4))
+        x_grouped_pool = ctx.enter_context(tc.tile_pool(name="x_grouped", bufs=4))
+        w_grouped_pool = ctx.enter_context(tc.tile_pool(name="w_grouped", bufs=2))
+        p_pool = ctx.enter_context(tc.tile_pool(name="p", bufs=8))
+        product_pool = ctx.enter_context(tc.tile_pool(name="product", bufs=1))
+        t2_pool = ctx.enter_context(tc.tile_pool(name="t2", bufs=4))
+        y01_pool = ctx.enter_context(tc.tile_pool(name="y01", bufs=5))
+        y2_pool = ctx.enter_context(tc.tile_pool(name="y2", bufs=2))
         psum = ctx.enter_context(tc.psum_pool(name="psum", bufs=1))
         ctx.enter_context(tc.manual_schedule())
 
-        dz = const.tile([P, 512], BF16, name="dz")
-        nc.vector.memset(dz[:], 0.0)
-        ident = const.tile([P, P], F32, name="ident")
-        masks.make_identity(nc, ident[:])
+        identity = const.tile([P, P], F32, name="identity")
+        masks.make_identity(nc, identity[:])
         ones = const.tile([P, P], F32, name="ones")
         nc.vector.memset(ones[:], 1.0)
-        warm = const.tile([P, 1], F32, name="warm")
-        nc.scalar.activation(out=warm[:], in_=ones[:, 0:1], func=ACT.Copy)
-        accs = const.tile([P, 12], F32, name="accs")
-        att_sb = const.tile([P, 6], F32, name="att_sb")
+        table_warm = const.tile([P, 1], F32, name="table_warm")
+        nc.scalar.activation(out=table_warm[:], in_=ones[:, 0:1], func=COPY)
+        pg_sums = const.tile([P, 12], F32, name="pg_sums")
+        att = const.tile([P, 6], F32, name="att")
 
         x_codes = {}
         x_scales = {}
-        for g in range(4):
-            x_codes[g] = keep.tile([P, 768], U32, name="xc%d" % g, align_bytes=64)
-            x_scales[g] = keep.tile([P, 768], U8, name="xs%d" % g, align_bytes=64)
-        wc = {}
-        ws = {}
-        for u in range(6):
-            wc[u] = keep.tile([P, 4, 512], U32, name="wc%d" % u, align_bytes=64)
-            ws[u] = keep.tile([P, 4, 512], U8, name="ws%d" % u, align_bytes=64)
+        for g in range(PASSES):
+            x_codes[g] = keep.tile([P, 768], U32, name="x_codes%d" % g, align_bytes=64)
+            x_scales[g] = keep.tile([P, 768], U8, name="x_scales%d" % g, align_bytes=64)
+        w_codes = {}
+        w_scales = {}
+        for u in range(len(units)):
+            w_codes[u] = keep.tile([P, PASSES, 512], U32, name="w_codes%d" % u, align_bytes=64)
+            w_scales[u] = keep.tile([P, PASSES, 512], U8, name="w_scales%d" % u, align_bytes=64)
+
         x_raw = {}
-        x_grp = {}
-        w_raw = {}
-        w_de = {}
-        grp = {}
-        tps = {}
-        p_sb = {}
-        t_sb = {}
-        state = {"d": 0}
+        raw = {}
+        reordered = {}
+        transposed = {}
+        w_grouped = {}
+        p_tiles = {}
+        t2_tiles = {}
+        groups_started = [0]
 
         def bank_tile(name, bank):
             return psum.tile([P, 512], F32, name=name, tag="bank%d" % bank)
 
-        def copy_on(eng, dst, src):
-            if eng == "S":
+        def next_sum_bank():
+            bank = FIRST_SUM_BANK + groups_started[0] % SUM_BANKS
+            groups_started[0] = groups_started[0] + 1
+            return bank
+
+        def copy_on(engine, dst, src):
+            if engine == "scalar":
                 nc.scalar.copy(out=dst, in_=src)
             else:
                 nc.vector.tensor_copy(out=dst, in_=src)
 
-        def scale_on(eng, dst, src, col):
-            if eng == "S":
-                nc.scalar.activation(out=dst, in_=src, func=ACT.Copy, scale=att_sb[:, col : col + 1])
+        def times_att(engine, dst, src, j, b):
+            factor = att[:, 3 * j + b : 3 * j + b + 1]
+            if engine == "scalar":
+                nc.scalar.activation(out=dst, in_=src, func=COPY, scale=factor)
             else:
-                nc.vector.tensor_scalar(
-                    out=dst, in0=src, scalar1=att_sb[:, col : col + 1], scalar2=None, op0=ALU.mult
+                nc.vector.tensor_scalar(out=dst, in0=src, scalar1=factor, scalar2=None, op0=MULT)
+
+        def load_strip(s):
+            matrix, j = units[s // 4]
+            row = j * 512 + (s % 4) * P
+            raw[s] = raw_pool.tile([P, 2048], BF16, name="raw%d" % s, tag="raw")
+            nc.sync.dma_start(out=raw[s][:], in_=matrix[row : row + P, :])
+
+        def load_x(b):
+            for g in range(PASSES):
+                x_raw[(b, g)] = keep.tile([P, 1024], BF16, name="x_raw%d_%d" % (b, g))
+                nc.sync.dma_start(
+                    out=x_raw[(b, g)][:],
+                    in_=x[b, g * 512 : (g + 1) * 512].rearrange("(q e) h w -> q (e h w)", e=4),
                 )
 
-        def op_d(n):
-            state["d"] = state["d"] + 1
-            dps = bank_tile("dummy%d" % state["d"], 5)
-            for i in range(n):
-                nc.tensor.matmul(out=dps[:], lhsT=dz[:, 0:P], rhs=dz[:], start=True, stop=True)
+        def quantise_x(b):
+            grouped = {}
+            for g in range(PASSES):
+                grouped[g] = x_grouped_pool.tile(
+                    [P, 1024], BF16, name="x_grouped%d_%d" % (b, g), tag="x_grouped", align_bytes=64
+                )
+                copy_on(
+                    "vector" if g < X_COPIES_ON_VECTOR[b] else "scalar",
+                    grouped[g][:].rearrange("q (n e) -> q n e", e=4),
+                    x_raw[(b, g)][:].rearrange("q (e n) -> q n e", e=4),
+                )
+            for g in range(PASSES):
+                cols = slice(b * 256, (b + 1) * 256)
+                nc.vector.quantize_mx(
+                    out=x_codes[g][:, cols].bitcast(E4M3_X4), scales=x_scales[g][:, cols], in_=grouped[g][:]
+                )
 
-        def op_lw(t):
-            w_ap, j = units[t // 4]
-            r0 = j * 512 + (t % 4) * P
-            w_raw[t] = wraw_pool.tile([P, 2048], BF16, name="wraw%d" % t, tag="wraw")
-            nc.sync.dma_start(out=w_raw[t][:], in_=w_ap[r0 : r0 + P, :])
-
-        def op_lx(b, g):
-            x_raw[(b, g)] = keep.tile([P, 1024], BF16, name="xraw%d_%d" % (b, g))
-            nc.sync.dma_start(
-                out=x_raw[(b, g)][:],
-                in_=x[b, g * 512 : (g + 1) * 512].rearrange("(p j) h w -> p (j h w)", j=4),
+        def reorder_strip(s):
+            reordered[s] = reordered_pool.tile([P, 1024], F32, name="reordered%d" % s, tag="reordered")
+            nc.vector.tensor_copy(
+                out=reordered[s][:].rearrange("c (g half q) -> c g half q", g=PASSES, half=2),
+                in_=raw[s][:].bitcast(F32).rearrange("c (g q half) -> c g half q", g=PASSES, half=2),
             )
 
-        def op_ix(b, g, eng):
-            x_grp[(b, g)] = xgrp_pool.tile([P, 1024], BF16, name="xgrp%d_%d" % (b, g), tag="xgrp", align_bytes=64)
-            copy_on(
-                eng,
-                x_grp[(b, g)][:].rearrange("p (n j) -> p n j", j=4),
-                x_raw[(b, g)][:].rearrange("p (j n) -> p n j", j=4),
-            )
+        def transpose_strip(s):
+            for i in range(2):
+                transposed[(s, i)] = bank_tile("transposed%d_%d" % (s, i), TRANSPOSE_BANKS[s % 2][i])
+                for slot in range(4):
+                    g, half = 2 * i + slot // 2, slot % 2
+                    if s >= FIRST_REORDERED:
+                        block = reordered[s][:, (2 * g + half) * P : (2 * g + half + 1) * P]
+                    else:
+                        block = raw[s][:].bitcast(F32)[:, 256 * g + half : 256 * (g + 1) : 2]
+                    nc.tensor.transpose(transposed[(s, i)][:, slot * P : (slot + 1) * P], block, identity[:])
 
-        def op_qx(b, g):
-            cols = slice(b * 256, (b + 1) * 256)
-            nc.vector.quantize_mx(
-                out=x_codes[g][:, cols].bitcast(E4), scales=x_scales[g][:, cols], in_=x_grp[(b, g)][:]
-            )
+        def empty_transposes(s):
+            u, sub = s // 4, s % 4
+            if sub == 0:
+                w_grouped[u] = w_grouped_pool.tile(
+                    [P, PASSES, 2048], BF16, name="w_grouped%d" % u, tag="w_grouped", align_bytes=64
+                )
+            words = w_grouped[u][:].bitcast(F32).rearrange("q g (c half) -> q g c half", half=2)
+            for i in range(2):
+                nc.scalar.copy(
+                    out=words[:, 2 * i : 2 * i + 2, sub * P : (sub + 1) * P, :],
+                    in_=transposed[(s, i)][:].rearrange("q (g half c) -> q g c half", g=2, half=2),
+                )
 
-        def op_pc(t, eng):
-            w_de[t] = wde_pool.tile([P, 1024], F32, name="wde%d" % t, tag="wde")
-            copy_on(
-                eng,
-                w_de[t][:].rearrange("c (g u p) -> c g u p", g=4, u=2),
-                w_raw[t][:].bitcast(F32).rearrange("c (g p u) -> c g u p", g=4, u=2),
-            )
+        def quantise_strip(s):
+            u, sub = s // 4, s % 4
+            channels = slice(sub * P, (sub + 1) * P)
+            for g in range(PASSES):
+                nc.vector.quantize_mx(
+                    out=w_codes[u][:, g, channels].bitcast(E5M2_X4),
+                    scales=w_scales[u][:, g, channels],
+                    in_=w_grouped[u][:, g, sub * 512 : (sub + 1) * 512],
+                )
 
-        def op_t(t, bank0, bank1, pre):
-            words = w_raw[t][:].bitcast(F32)
-            for h, bank in ((0, bank0), (1, bank1)):
-                tp = bank_tile("tp%d_%d" % (t, h), bank)
-                tps[(t, h)] = tp
-                for gl in range(2):
-                    g = 2 * h + gl
-                    for u in range(2):
-                        s = 2 * gl + u
-                        if pre:
-                            src = w_de[t][:, (2 * g + u) * P : (2 * g + u + 1) * P]
-                        else:
-                            src = words[:, 256 * g + u : 256 * (g + 1) : 2]
-                        nc.tensor.transpose(tp[:, s * P : (s + 1) * P], src, ident[:])
+        def quantise_unit(u):
+            for g in range(PASSES):
+                nc.vector.quantize_mx(
+                    out=w_codes[u][:, g, :].bitcast(E5M2_X4), scales=w_scales[u][:, g, :], in_=w_grouped[u][:, g, :]
+                )
 
-        def op_ev(t, h, eng, bank):
-            u, cb = t // 4, t % 4
-            if cb == 0 and h == 0:
-                grp[u] = grp_pool.tile([P, 4, 2048], BF16, name="grp%d" % u, tag="grp", align_bytes=64)
-            gw = grp[u][:].bitcast(F32).rearrange("p g (c u) -> p g c u", u=2)
-            copy_on(
-                eng,
-                gw[:, 2 * h : 2 * h + 2, cb * P : (cb + 1) * P, :],
-                tps[(t, h)][:].rearrange("p (g u c) -> p g c u", g=2, u=2),
-            )
-
-        def op_qu(u, g):
-            nc.vector.quantize_mx(out=wc[u][:, g, :].bitcast(E5), scales=ws[u][:, g, :], in_=grp[u][:, g, :])
-
-        def op_qc(t, g):
-            u, cb = t // 4, t % 4
-            ch = slice(cb * P, (cb + 1) * P)
-            nc.vector.quantize_mx(
-                out=wc[u][:, g, ch].bitcast(E5),
-                scales=ws[u][:, g, ch],
-                in_=grp[u][:, g, cb * 512 : (cb + 1) * 512],
-            )
-
-        def op_gb(u, m, eng, bank):
-            acc = bank_tile("acc%d_%d" % (u, m), bank)
+        def positions_by_channels(u, m):
+            sums = bank_tile("sums%d_%d" % (u, m), next_sum_bank())
             cols = slice(m * P, (m + 1) * P)
-            for g in range(4):
+            for g in range(PASSES):
                 nc.tensor.matmul_mx(
-                    out=acc[:],
-                    lhsT=x_codes[g][:, cols].bitcast(E4),
+                    out=sums[:],
+                    lhsT=x_codes[g][:, cols].bitcast(E4M3_X4),
                     lhsT_scale=x_scales[g][:, cols],
-                    rhs=wc[u][:, g, :].bitcast(E5),
-                    rhs_scale=ws[u][:, g, :],
+                    rhs=w_codes[u][:, g, :].bitcast(E5M2_X4),
+                    rhs_scale=w_scales[u][:, g, :],
                     start=(g == 0),
-                    stop=(g == 3),
+                    stop=(g == PASSES - 1),
                 )
-            j = units[u][1]
-            if u >= 4:
-                t_sb[(u, m)] = tt_pool.tile([P, 512], F32, name="tsb%d_%d" % (u, m), tag="tsb")
-                scale_on(eng, t_sb[(u, m)][:], acc[:], 3 * j + 2)
-            elif u % 2 == 0:
-                p_sb[(j, m)] = psb_pool.tile([P, 512], F32, name="psb%d_%d" % (j, m), tag="psb")
-                copy_on(eng, p_sb[(j, m)][:], acc[:])
-            else:
-                junk = junk_pool.tile([P, 512], F32, name="junk%d_%d" % (j, m), tag="junk")
-                nc.vector.scalar_tensor_tensor(
-                    out=junk[:],
-                    in0=acc[:],
-                    scalar=1.0,
-                    in1=p_sb[(j, m)][:],
-                    op0=ALU.mult,
-                    op1=ALU.mult,
-                    accum_out=accs[:, 6 * j + m : 6 * j + m + 1],
-                )
+            return sums
 
-        def op_att(j, bank):
-            att_ps = bank_tile("attps%d" % j, bank)
+        def p_group(u, m):
+            j = units[u][1]
+            sums = positions_by_channels(u, m)
+            p_tiles[(j, m)] = p_pool.tile([P, 512], F32, name="p%d_%d" % (j, m), tag="p")
+            nc.scalar.copy(out=p_tiles[(j, m)][:], in_=sums[:])
+
+        def g_group(u, m):
+            j = units[u][1]
+            sums = positions_by_channels(u, m)
+            product = product_pool.tile([P, 512], F32, name="product%d_%d" % (j, m), tag="product")
+            nc.vector.scalar_tensor_tensor(
+                out=product[:],
+                in0=sums[:],
+                scalar=1.0,
+                in1=p_tiles[(j, m)][:],
+                op0=MULT,
+                op1=MULT,
+                accum_out=pg_sums[:, 6 * j + m : 6 * j + m + 1],
+            )
+
+        def attention(j):
+            totals = bank_tile("totals%d" % j, next_sum_bank())
             nc.tensor.matmul(
-                out=att_ps[:, 0:6], lhsT=ones[:], rhs=accs[:, 6 * j : 6 * j + 6], start=True, stop=True
+                out=totals[:, 0:6], lhsT=ones[:], rhs=pg_sums[:, 6 * j : 6 * j + 6], start=True, stop=True
             )
             nc.vector.tensor_reduce(
-                out=att_sb[:, 3 * j : 3 * j + 3],
-                in_=att_ps[:, 0:6].rearrange("p (b h) -> p b h", h=2),
-                axis=AX.X,
-                op=ALU.add,
+                out=att[:, 3 * j : 3 * j + 3],
+                in_=totals[:, 0:6].rearrange("q (b h) -> q b h", h=2),
+                axis=mybir.AxisListType.X,
+                op=ADD,
             )
 
-        def op_ga(u, cb, eng, bank):
+        def t_image2_group(u, m, engine):
             j = units[u][1]
-            acc = bank_tile("acct%d_%d" % (u, cb), bank)
-            ch = slice(cb * P, (cb + 1) * P)
-            for g in range(4):
+            sums = positions_by_channels(u, m)
+            t2_tiles[(u, m)] = t2_pool.tile([P, 512], F32, name="t2_%d_%d" % (u, m), tag="t2")
+            times_att(engine, t2_tiles[(u, m)][:], sums[:], j, 2)
+
+        def t_image2_back(u):
+            j = units[u][1]
+            for pair in range(2):
+                turned = bank_tile("turned%d_%d" % (u, pair), next_sum_bank())
+                for slot in range(4):
+                    sub, h = 2 * pair + slot // 2, slot % 2
+                    nc.tensor.transpose(
+                        turned[:, slot * P : (slot + 1) * P],
+                        t2_tiles[(u, 4 + h)][:, sub * P : (sub + 1) * P],
+                        identity[:],
+                    )
+                y2 = y2_pool.tile([P, 2, 256], F32, name="y2_%d_%d" % (u, pair), tag="y2")
+                nc.vector.tensor_copy(out=y2[:].rearrange("c l n -> c (l n)"), in_=turned[:])
+                nc.sync.dma_start(
+                    out=out[2, j, pair * 256 : (pair + 1) * 256, :].rearrange("(l c) n -> c l n", l=2), in_=y2[:]
+                )
+
+        def t_images01_group(u, sub, engine):
+            j = units[u][1]
+            sums = bank_tile("sums01_%d_%d" % (u, sub), next_sum_bank())
+            channels = slice(sub * P, (sub + 1) * P)
+            for g in range(PASSES):
                 nc.tensor.matmul_mx(
-                    out=acc[:],
-                    lhsT=wc[u][:, g, ch].bitcast(E5),
-                    lhsT_scale=ws[u][:, g, ch],
-                    rhs=x_codes[g][:, 0:512].bitcast(E4),
+                    out=sums[:],
+                    lhsT=w_codes[u][:, g, channels].bitcast(E5M2_X4),
+                    lhsT_scale=w_scales[u][:, g, channels],
+                    rhs=x_codes[g][:, 0:512].bitcast(E4M3_X4),
                     rhs_scale=x_scales[g][:, 0:512],
                     start=(g == 0),
-                    stop=(g == 3),
+                    stop=(g == PASSES - 1),
                 )
-            o01 = o01_pool.tile([P, 2, 256], F32, name="o01_%d_%d" % (u, cb), tag="o01")
+            y01 = y01_pool.tile([P, 2, 256], F32, name="y01_%d_%d" % (u, sub), tag="y01")
             for b in range(2):
-                scale_on(eng, o01[:, b, :], acc[:, b * 256 : (b + 1) * 256], 3 * j + b)
-            nc.sync.dma_start(out=out[0:2, j, ch, :].rearrange("b c n -> c b n"), in_=o01[:])
+                times_att(engine, y01[:, b, :], sums[:, b * 256 : (b + 1) * 256], j, b)
+            nc.sync.dma_start(out=out[0:2, j, channels, :].rearrange("b c n -> c b n"), in_=y01[:])
 
-        def op_bt(u, half, bank):
-            tp = bank_tile("bt%d_%d" % (u, half), bank)
-            tps[("bt", u, half)] = tp
-            for l in range(2):
-                cb = 2 * half + l
-                for mh in range(2):
-                    s = 2 * l + mh
-                    nc.tensor.transpose(
-                        tp[:, s * P : (s + 1) * P], t_sb[(u, 4 + mh)][:, cb * P : (cb + 1) * P], ident[:]
-                    )
+        def multiply_half_unit(k):
+            u, second = k // 2, k % 2
+            if u < 4:
+                for m in range(3 * second, 3 * second + 3):
+                    if u % 2 == 0:
+                        p_group(u, m)
+                    else:
+                        g_group(u, m)
+            elif second == 0:
+                t_image2_group(u, 4, "scalar")
+                t_image2_group(u, 5, "vector")
+                t_images01_group(u, 0, "scalar")
+            else:
+                t_images01_group(u, 1, "vector")
+                t_images01_group(u, 2, "scalar")
+                t_images01_group(u, 3, "vector")
 
-        def op_eb(u, half, eng, bank):
-            j = units[u][1]
-            o2 = o2_pool.tile([P, 2, 256], F32, name="o2_%d_%d" % (u, half), tag="o2")
-            copy_on(eng, o2[:].rearrange("c l n -> c (l n)"), tps[("bt", u, half)][:])
-            nc.sync.dma_start(
-                out=out[2, j, half * 256 : (half + 1) * 256, :].rearrange("(l c) n -> c l n", l=2), in_=o2[:]
-            )
+        def transpose_round(r):
+            for s in (2 * r, 2 * r + 1):
+                transpose_strip(s)
+                empty_transposes(s)
+                if s + RAW_BUFS < STRIPS:
+                    load_strip(s + RAW_BUFS)
+                if s < STRIPWISE_QUANTISED:
+                    quantise_strip(s)
+            if r == ROUNDS - 1:
+                t_image2_back(T_UNITS[0])
+            for s in (2 * r + 2, 2 * r + 3):
+                if FIRST_REORDERED + 2 <= s < STRIPS:
+                    reorder_strip(s)
+            if r % 2 == 1 and 2 * r + 1 >= STRIPWISE_QUANTISED:
+                quantise_unit(r // 2)
 
-        table = {
-            "LW": op_lw, "LX": op_lx, "IX": op_ix, "QX": op_qx, "PC": op_pc, "T": op_t, "EV": op_ev,
-            "QU": op_qu, "D": op_d, "QC": op_qc, "GB": op_gb, "ATT": op_att, "GA": op_ga, "BT": op_bt, "EB": op_eb,
-        }
-        for step in plan:
-            table[step[0]](*step[1:])
+        for s in range(4):
+            load_strip(s)
+        load_x(0)
+        for s in range(4, RAW_BUFS):
+            load_strip(s)
+        load_x(1)
+        transpose_round(0)
+        load_x(2)
+        transpose_round(1)
+        quantise_x(0)
+        transpose_round(2)
+        transpose_round(3)
+        quantise_x(1)
+        for m in (0, 1):
+            p_group(0, m)
+        for m in (0, 1):
+            g_group(1, m)
+        reorder_strip(FIRST_REORDERED)
+        reorder_strip(FIRST_REORDERED + 1)
+        quantise_x(2)
+        for m in (2, 3):
+            p_group(0, m)
+        for m in (2, 3):
+            g_group(1, m)
+        transpose_round(4)
+        for m in (4, 5):
+            p_group(0, m)
+        transpose_round(5)
+        for m in (4, 5):
+            g_group(1, m)
+
+        for r in range(FIRST_REGULAR_ROUND, ROUNDS + BLOCK_LAG):
+            if r in ATT_ROUND:
+                attention(ATT_ROUND[r])
+            if r < ROUNDS:
+                transpose_round(r)
+            multiply_half_unit(r - BLOCK_LAG)
+            if r == ROUNDS:
+                t_image2_back(T_UNITS[1])

@@ -63,13 +63,13 @@ def tile_spatialcgnl_pa_kernel(tc, x, Wt, Wp, Wg, out):
         x_codes = {}
         x_scales = {}
         for g in range(PASSES):
-            x_codes[g] = keep.tile([P, 768], U32, name="x_codes%d" % g, align_bytes=64)
-            x_scales[g] = keep.tile([P, 768], U8, name="x_scales%d" % g, align_bytes=64)
+            x_codes[g] = keep.tile([P, 768], U32, name="x_codes%d" % g, align_bytes=256)
+            x_scales[g] = keep.tile([P, 768], U8, name="x_scales%d" % g, align_bytes=256)
         w_codes = {}
         w_scales = {}
         for u in range(len(units)):
-            w_codes[u] = keep.tile([P, PASSES, 512], U32, name="w_codes%d" % u, align_bytes=64)
-            w_scales[u] = keep.tile([P, PASSES, 512], U8, name="w_scales%d" % u, align_bytes=64)
+            w_codes[u] = keep.tile([P, PASSES, 512], U32, name="w_codes%d" % u, align_bytes=256)
+            w_scales[u] = keep.tile([P, PASSES, 512], U8, name="w_scales%d" % u, align_bytes=256)
 
         x_raw = {}
         raw = {}

@@ -29,6 +29,7 @@ X_COPIES_ON_VECTOR = (3, 3, 2)
 FIRST_REGULAR_ROUND = 6
 BLOCK_LAG = 2
 ATT_ROUND = {7: 0, 11: 1}
+RUN = 4
 T_UNITS = (4, 5)
 
 
@@ -123,8 +124,8 @@ def tile_spatialcgnl_pa_kernel(tc, x, Wt, Wp, Wg, out):
                 )
                 copy_on(
                     "vector" if g < X_COPIES_ON_VECTOR[b] else "scalar",
-                    grouped[g][:].rearrange("q (n e) -> q n e", e=4),
-                    x_raw[(b, g)][:].rearrange("q (e n) -> q n e", e=4),
+                    grouped[g][:].rearrange("q (c i e) -> q c e i", i=RUN, e=4),
+                    x_raw[(b, g)][:].rearrange("q (e c i) -> q c e i", i=RUN, e=4),
                 )
             for g in range(PASSES):
                 cols = slice(b * 256, (b + 1) * 256)

@@ -17,7 +17,8 @@ ADD = mybir.AluOpType.add
 
 P = 128
 PASSES = 4
-STRIPS = 24
+STRIPS = 20
+CHUNK_UNIT = 5
 ROUNDS = STRIPS // 2
 RAW_BUFS = 8
 FIRST_REORDERED = 8
@@ -42,13 +43,16 @@ def tile_spatialcgnl_pa_kernel(tc, x, Wt, Wp, Wg, out):
         keep = ctx.enter_context(tc.tile_pool(name="keep", bufs=1))
         raw_pool = ctx.enter_context(tc.tile_pool(name="raw", bufs=RAW_BUFS))
         reordered_pool = ctx.enter_context(tc.tile_pool(name="reordered", bufs=4))
+        turned_pool = ctx.enter_context(tc.tile_pool(name="turned_chunk", bufs=2))
         x_grouped_pool = ctx.enter_context(tc.tile_pool(name="x_grouped", bufs=4))
-        w_grouped_pool = ctx.enter_context(tc.tile_pool(name="w_grouped", bufs=2))
+        w_grouped_pool = ctx.enter_context(tc.tile_pool(name="w_grouped", bufs=3))
+        x_raw_pool = ctx.enter_context(tc.tile_pool(name="x_raw", bufs=8))
         p_pool = ctx.enter_context(tc.tile_pool(name="p", bufs=8))
         product_pool = ctx.enter_context(tc.tile_pool(name="product", bufs=1))
         t2_pool = ctx.enter_context(tc.tile_pool(name="t2", bufs=4))
         y01_pool = ctx.enter_context(tc.tile_pool(name="y01", bufs=5))
-        y2_pool = ctx.enter_context(tc.tile_pool(name="y2", bufs=2))
+        chunk_grouped_pool = ctx.enter_context(tc.tile_pool(name="chunk_grouped", bufs=2))
+        y2_pool = ctx.enter_context(tc.tile_pool(name="y2", bufs=4))
         psum = ctx.enter_context(tc.psum_pool(name="psum", bufs=1))
         ctx.enter_context(tc.manual_schedule())
 
@@ -75,6 +79,10 @@ def tile_spatialcgnl_pa_kernel(tc, x, Wt, Wp, Wg, out):
         x_raw = {}
         raw = {}
         reordered = {}
+        chunk_raw = {}
+        chunk_reordered = {}
+        chunk_turned = {}
+        chunk_grouped = {}
         transposed = {}
         w_grouped = {}
         p_tiles = {}
@@ -108,9 +116,47 @@ def tile_spatialcgnl_pa_kernel(tc, x, Wt, Wp, Wg, out):
             raw[s] = raw_pool.tile([P, 2048], BF16, name="raw%d" % s, tag="raw")
             nc.sync.dma_start(out=raw[s][:], in_=matrix[row : row + P, :])
 
+        def load_chunk(g):
+            matrix, j = units[CHUNK_UNIT]
+            chunk_raw[g] = raw_pool.tile([P, 2048], BF16, name="chunk_raw%d" % g, tag="raw")
+            for z in range(4):
+                k = slice(512 * g + 128 * z, 512 * g + 128 * (z + 1))
+                nc.sync.dma_start(
+                    out=chunk_raw[g][32 * z : 32 * (z + 1), :].rearrange("r (i w) -> r i w", i=16),
+                    in_=matrix[j * 512 : (j + 1) * 512, k].rearrange("(i r) w -> r i w", r=32),
+                )
+
+        def reorder_chunk(g, engine="vector"):
+            chunk_reordered[g] = reordered_pool.tile([P, 1024], F32, name="chunk_reordered%d" % g, tag="reordered", align_bytes=64)
+            copy_on(
+                engine,
+                chunk_reordered[g][:].rearrange("c (i half q) -> c i half q", i=16, half=2),
+                chunk_raw[g][:].bitcast(F32).rearrange("c (i q half) -> c i half q", i=16, half=2),
+            )
+
+        def turn_chunk(g):
+            chunk_turned[g] = turned_pool.tile([P, 1024], F32, name="chunk_turned%d" % g, tag="turned_chunk", align_bytes=64)
+            nc.vector.transpose(out=chunk_turned[g][:], in_=chunk_reordered[g][:])
+
+        def group_chunk(g, engine="scalar"):
+            chunk_grouped[g] = chunk_grouped_pool.tile(
+                [P, 2048], BF16, name="chunk_grouped%d" % g, tag="chunk_grouped", align_bytes=64
+            )
+            copy_on(
+                engine,
+                chunk_grouped[g][:].bitcast(F32).rearrange("q (i r half) -> q i r half", i=16, half=2),
+                chunk_turned[g][:].rearrange("q (i half r) -> q i r half", i=16, half=2),
+            )
+
+        def quantise_chunk(g):
+            u = CHUNK_UNIT
+            nc.vector.quantize_mx(
+                out=w_codes[u][:, g, :].bitcast(E5M2_X4), scales=w_scales[u][:, g, :], in_=chunk_grouped[g][:]
+            )
+
         def load_x(b):
             for g in range(PASSES):
-                x_raw[(b, g)] = keep.tile([P, 1024], BF16, name="x_raw%d_%d" % (b, g))
+                x_raw[(b, g)] = x_raw_pool.tile([P, 1024], BF16, name="x_raw%d_%d" % (b, g), tag="x_raw")
                 nc.sync.dma_start(
                     out=x_raw[(b, g)][:],
                     in_=x[b, g * 512 : (g + 1) * 512].rearrange("(q e) h w -> q (e h w)", e=4),
@@ -134,7 +180,7 @@ def tile_spatialcgnl_pa_kernel(tc, x, Wt, Wp, Wg, out):
                 )
 
         def reorder_strip(s):
-            reordered[s] = reordered_pool.tile([P, 1024], F32, name="reordered%d" % s, tag="reordered")
+            reordered[s] = reordered_pool.tile([P, 1024], F32, name="reordered%d" % s, tag="reordered", align_bytes=64)
             nc.vector.tensor_copy(
                 out=reordered[s][:].rearrange("c (g half q) -> c g half q", g=PASSES, half=2),
                 in_=raw[s][:].bitcast(F32).rearrange("c (g q half) -> c g half q", g=PASSES, half=2),
@@ -152,12 +198,12 @@ def tile_spatialcgnl_pa_kernel(tc, x, Wt, Wp, Wg, out):
                     nc.tensor.transpose(transposed[(s, i)][:, slot * P : (slot + 1) * P], block, identity[:])
 
         def empty_transposes(s):
-            u, sub = s // 4, s % 4
+            pair, sub = s // 2, s % 2
             if sub == 0:
-                w_grouped[u] = w_grouped_pool.tile(
-                    [P, PASSES, 2048], BF16, name="w_grouped%d" % u, tag="w_grouped", align_bytes=64
+                w_grouped[pair] = w_grouped_pool.tile(
+                    [P, PASSES, 1024], BF16, name="w_grouped%d" % pair, tag="w_grouped", align_bytes=64
                 )
-            words = w_grouped[u][:].bitcast(F32).rearrange("q g (c half) -> q g c half", half=2)
+            words = w_grouped[pair][:].bitcast(F32).rearrange("q g (c half) -> q g c half", half=2)
             for i in range(2):
                 nc.scalar.copy(
                     out=words[:, 2 * i : 2 * i + 2, sub * P : (sub + 1) * P, :],
@@ -171,13 +217,16 @@ def tile_spatialcgnl_pa_kernel(tc, x, Wt, Wp, Wg, out):
                 nc.vector.quantize_mx(
                     out=w_codes[u][:, g, channels].bitcast(E5M2_X4),
                     scales=w_scales[u][:, g, channels],
-                    in_=w_grouped[u][:, g, sub * 512 : (sub + 1) * 512],
+                    in_=w_grouped[s // 2][:, g, s % 2 * 512 : (s % 2 + 1) * 512],
                 )
 
-        def quantise_unit(u):
+        def quantise_pair(r):
+            u = r // 2
+            channels = slice((r % 2) * 256, (r % 2 + 1) * 256)
             for g in range(PASSES):
                 nc.vector.quantize_mx(
-                    out=w_codes[u][:, g, :].bitcast(E5M2_X4), scales=w_scales[u][:, g, :], in_=w_grouped[u][:, g, :]
+                    out=w_codes[u][:, g, channels].bitcast(E5M2_X4), scales=w_scales[u][:, g, channels],
+                    in_=w_grouped[r][:, g, :],
                 )
 
         def positions_by_channels(u, m):
@@ -269,38 +318,22 @@ def tile_spatialcgnl_pa_kernel(tc, x, Wt, Wp, Wg, out):
                 times_att(engine, y01[:, b, :], sums[:, b * 256 : (b + 1) * 256], j, b)
             nc.sync.dma_start(out=out[0:2, j, channels, :].rearrange("b c n -> c b n"), in_=y01[:])
 
-        def multiply_half_unit(k):
-            u, second = k // 2, k % 2
-            if u < 4:
-                for m in range(3 * second, 3 * second + 3):
-                    if u % 2 == 0:
-                        p_group(u, m)
-                    else:
-                        g_group(u, m)
-            elif second == 0:
-                t_image2_group(u, 4, "scalar")
-                t_image2_group(u, 5, "vector")
-                t_images01_group(u, 0, "scalar")
-            else:
-                t_images01_group(u, 1, "vector")
-                t_images01_group(u, 2, "scalar")
-                t_images01_group(u, 3, "vector")
+        later_loads = [(load_strip, 8), (load_strip, 9), (load_strip, 10), (load_strip, 11), (load_strip, 12), (load_strip, 13), (load_chunk, 0), (load_strip, 14), (load_strip, 15), (load_chunk, 1), (load_strip, 16), (load_strip, 17), (load_chunk, 2), (load_strip, 18), (load_strip, 19), (load_chunk, 3)]
 
         def transpose_round(r):
             for s in (2 * r, 2 * r + 1):
                 transpose_strip(s)
                 empty_transposes(s)
-                if s + RAW_BUFS < STRIPS:
-                    load_strip(s + RAW_BUFS)
+                if s < len(later_loads):
+                    load, which = later_loads[s]
+                    load(which)
                 if s < STRIPWISE_QUANTISED:
                     quantise_strip(s)
-            if r == ROUNDS - 1:
-                t_image2_back(T_UNITS[0])
             for s in (2 * r + 2, 2 * r + 3):
                 if FIRST_REORDERED + 2 <= s < STRIPS:
                     reorder_strip(s)
-            if r % 2 == 1 and 2 * r + 1 >= STRIPWISE_QUANTISED:
-                quantise_unit(r // 2)
+            if r in (4, 5):
+                quantise_pair(r)
 
         for s in range(4):
             load_strip(s)
@@ -309,9 +342,9 @@ def tile_spatialcgnl_pa_kernel(tc, x, Wt, Wp, Wg, out):
             load_strip(s)
         load_x(1)
         transpose_round(0)
-        load_x(2)
         transpose_round(1)
         quantise_x(0)
+        load_x(2)
         transpose_round(2)
         transpose_round(3)
         quantise_x(1)
@@ -333,11 +366,60 @@ def tile_spatialcgnl_pa_kernel(tc, x, Wt, Wp, Wg, out):
         for m in (4, 5):
             g_group(1, m)
 
-        for r in range(FIRST_REGULAR_ROUND, ROUNDS + BLOCK_LAG):
-            if r in ATT_ROUND:
-                attention(ATT_ROUND[r])
-            if r < ROUNDS:
-                transpose_round(r)
-            multiply_half_unit(r - BLOCK_LAG)
-            if r == ROUNDS:
-                t_image2_back(T_UNITS[1])
+        for r in range(FIRST_REGULAR_ROUND, ROUNDS):
+            if r == 7:
+                attention(0)
+            transpose_round(r)
+            h = r - BLOCK_LAG
+            u, second = h // 2, h % 2
+            first = 3 * second
+            if r == 6:
+                reorder_chunk(0)
+                turn_chunk(0)
+                for m in range(first, first + 3):
+                    p_group(u, m)
+                group_chunk(0)
+                quantise_pair(6)
+                reorder_chunk(1)
+            if r == 7:
+                turn_chunk(1)
+                p_group(u, 3)
+                p_group(u, 4)
+                p_group(u, 5)
+                quantise_chunk(0)
+                quantise_pair(7)
+                group_chunk(1)
+            if r == 8:
+                g_group(u, 0)
+                reorder_chunk(2)
+                g_group(u, 1)
+                quantise_pair(8)
+                g_group(u, 2)
+                quantise_chunk(1)
+            if r == 9:
+                turn_chunk(2)
+                group_chunk(2)
+                g_group(u, 3)
+                g_group(u, 4)
+                quantise_pair(9)
+                g_group(u, 5)
+        for sub in (0, 1):
+            t_images01_group(4, sub, "scalar")
+        reorder_chunk(3)
+        turn_chunk(3)
+        quantise_chunk(2)
+        group_chunk(3)
+        attention(1)
+        t_images01_group(4, 2, "vector")
+        t_images01_group(4, 3, "scalar")
+        quantise_chunk(3)
+        t_image2_group(4, 4, "scalar")
+        t_image2_group(4, 5, "vector")
+        t_image2_group(5, 4, "scalar")
+        t_image2_group(5, 5, "vector")
+        t_images01_group(5, 0, "scalar")
+        t_images01_group(5, 1, "vector")
+        t_image2_back(4)
+        t_image2_back(5)
+        t_images01_group(5, 2, "scalar")
+        t_images01_group(5, 3, "vector")

@@ -46,8 +46,8 @@ def tile_spatialcgnl_pa_kernel(tc, x, Wt, Wp, Wg, out):
         turned_pool = ctx.enter_context(tc.tile_pool(name="turned_chunk", bufs=2))
         x_grouped_pool = ctx.enter_context(tc.tile_pool(name="x_grouped", bufs=4))
         w_grouped_pool = ctx.enter_context(tc.tile_pool(name="w_grouped", bufs=3))
-        x_raw_pool = ctx.enter_context(tc.tile_pool(name="x_raw", bufs=8))
-        p_pool = ctx.enter_context(tc.tile_pool(name="p", bufs=8))
+        x_raw_pool = ctx.enter_context(tc.tile_pool(name="x_raw", bufs=4))
+        p_pool = ctx.enter_context(tc.tile_pool(name="p", bufs=7))
         product_pool = ctx.enter_context(tc.tile_pool(name="product", bufs=1))
         t2_pool = ctx.enter_context(tc.tile_pool(name="t2", bufs=4))
         y01_pool = ctx.enter_context(tc.tile_pool(name="y01", bufs=5))
@@ -118,10 +118,10 @@ def tile_spatialcgnl_pa_kernel(tc, x, Wt, Wp, Wg, out):
 
         def load_chunk(g):
             matrix, j = units[CHUNK_UNIT]
-            chunk_raw[g] = raw_pool.tile([P, 2048], BF16, name="chunk_raw%d" % g, tag="raw")
+            chunk_raw[g] = x_raw_pool.tile([P, 2048], BF16, name="chunk_raw%d" % g, tag="x_raw")
             for z in range(4):
                 k = slice(512 * g + 128 * z, 512 * g + 128 * (z + 1))
-                nc.sync.dma_start(
+                nc.gpsimd.dma_start(
                     out=chunk_raw[g][32 * z : 32 * (z + 1), :].rearrange("r (i w) -> r i w", i=16),
                     in_=matrix[j * 512 : (j + 1) * 512, k].rearrange("(i r) w -> r i w", r=32),
                 )
@@ -156,9 +156,11 @@ def tile_spatialcgnl_pa_kernel(tc, x, Wt, Wp, Wg, out):
 
         def load_x(b):
             for g in range(PASSES):
-                x_raw[(b, g)] = x_raw_pool.tile([P, 1024], BF16, name="x_raw%d_%d" % (b, g), tag="x_raw")
+                if g % 2 == 0:
+                    two_passes = x_raw_pool.tile([P, 2048], BF16, name="x_raw%d_%d" % (b, g), tag="x_raw")
+                x_raw[(b, g)] = two_passes[:, g % 2 * 1024 : (g % 2 + 1) * 1024]
                 nc.sync.dma_start(
-                    out=x_raw[(b, g)][:],
+                    out=x_raw[(b, g)],
                     in_=x[b, g * 512 : (g + 1) * 512].rearrange("(q e) h w -> q (e h w)", e=4),
                 )
 
@@ -171,7 +173,7 @@ def tile_spatialcgnl_pa_kernel(tc, x, Wt, Wp, Wg, out):
                 copy_on(
                     "vector" if g < X_COPIES_ON_VECTOR[b] else "scalar",
                     grouped[g][:].rearrange("q (c i e) -> q c e i", i=RUN, e=4),
-                    x_raw[(b, g)][:].rearrange("q (e c i) -> q c e i", i=RUN, e=4),
+                    x_raw[(b, g)].rearrange("q (e c i) -> q c e i", i=RUN, e=4),
                 )
             for g in range(PASSES):
                 cols = slice(b * 256, (b + 1) * 256)
@@ -318,15 +320,12 @@ def tile_spatialcgnl_pa_kernel(tc, x, Wt, Wp, Wg, out):
                 times_att(engine, y01[:, b, :], sums[:, b * 256 : (b + 1) * 256], j, b)
             nc.sync.dma_start(out=out[0:2, j, channels, :].rearrange("b c n -> c b n"), in_=y01[:])
 
-        later_loads = [(load_strip, 8), (load_strip, 9), (load_strip, 10), (load_strip, 11), (load_strip, 12), (load_strip, 13), (load_chunk, 0), (load_strip, 14), (load_strip, 15), (load_chunk, 1), (load_strip, 16), (load_strip, 17), (load_chunk, 2), (load_strip, 18), (load_strip, 19), (load_chunk, 3)]
-
         def transpose_round(r):
             for s in (2 * r, 2 * r + 1):
                 transpose_strip(s)
                 empty_transposes(s)
-                if s < len(later_loads):
-                    load, which = later_loads[s]
-                    load(which)
+                if s + RAW_BUFS < STRIPS:
+                    load_strip(s + RAW_BUFS)
                 if s < STRIPWISE_QUANTISED:
                     quantise_strip(s)
             for s in (2 * r + 2, 2 * r + 3):
@@ -348,6 +347,8 @@ def tile_spatialcgnl_pa_kernel(tc, x, Wt, Wp, Wg, out):
         transpose_round(2)
         transpose_round(3)
         quantise_x(1)
+        load_chunk(0)
+        load_chunk(1)
         for m in (0, 1):
             p_group(0, m)
         for m in (0, 1):
@@ -355,6 +356,8 @@ def tile_spatialcgnl_pa_kernel(tc, x, Wt, Wp, Wg, out):
         reorder_strip(FIRST_REORDERED)
         reorder_strip(FIRST_REORDERED + 1)
         quantise_x(2)
+        load_chunk(2)
+        load_chunk(3)
         for m in (2, 3):
             p_group(0, m)
         for m in (2, 3):

@@ -23,9 +23,9 @@ ROUNDS = STRIPS // 2
 RAW_BUFS = 8
 FIRST_REORDERED = 8
 STRIPWISE_QUANTISED = 8
-TRANSPOSE_BANKS = ((6, 7), (0, 1))
-FIRST_SUM_BANK = 2
-SUM_BANKS = 4
+TRANSPOSE_BANKS = ((6, 7), (0, 1), (2, 3), (4, 5))
+SUM_BANKS = (2, 3, 4, 5)
+LATE_SUM_BANKS = (6, 7, 0, 1, 2, 3, 4, 5)
 X_COPIES_ON_VECTOR = (3, 3, 2)
 FIRST_REGULAR_ROUND = 6
 BLOCK_LAG = 2
@@ -87,14 +87,14 @@ def tile_spatialcgnl_pa_kernel(tc, x, Wt, Wp, Wg, out):
         w_grouped = {}
         p_tiles = {}
         t2_tiles = {}
-        groups_started = [0]
+        sum_ring = {"banks": SUM_BANKS, "next": 0}
 
         def bank_tile(name, bank):
             return psum.tile([P, 512], F32, name=name, tag="bank%d" % bank)
 
         def next_sum_bank():
-            bank = FIRST_SUM_BANK + groups_started[0] % SUM_BANKS
-            groups_started[0] = groups_started[0] + 1
+            bank = sum_ring["banks"][sum_ring["next"] % len(sum_ring["banks"])]
+            sum_ring["next"] = sum_ring["next"] + 1
             return bank
 
         def copy_on(engine, dst, src):
@@ -116,12 +116,12 @@ def tile_spatialcgnl_pa_kernel(tc, x, Wt, Wp, Wg, out):
             raw[s] = raw_pool.tile([P, 2048], BF16, name="raw%d" % s, tag="raw")
             nc.sync.dma_start(out=raw[s][:], in_=matrix[row : row + P, :])
 
-        def load_chunk(g):
+        def load_chunk(g, queue):
             matrix, j = units[CHUNK_UNIT]
             chunk_raw[g] = x_raw_pool.tile([P, 2048], BF16, name="chunk_raw%d" % g, tag="x_raw")
             for z in range(4):
                 k = slice(512 * g + 128 * z, 512 * g + 128 * (z + 1))
-                nc.gpsimd.dma_start(
+                queue.dma_start(
                     out=chunk_raw[g][32 * z : 32 * (z + 1), :].rearrange("r (i w) -> r i w", i=16),
                     in_=matrix[j * 512 : (j + 1) * 512, k].rearrange("(i r) w -> r i w", r=32),
                 )
@@ -190,7 +190,7 @@ def tile_spatialcgnl_pa_kernel(tc, x, Wt, Wp, Wg, out):
 
         def transpose_strip(s):
             for i in range(2):
-                transposed[(s, i)] = bank_tile("transposed%d_%d" % (s, i), TRANSPOSE_BANKS[s % 2][i])
+                transposed[(s, i)] = bank_tile("transposed%d_%d" % (s, i), TRANSPOSE_BANKS[s % (4 if s < STRIPWISE_QUANTISED else 2)][i])
                 for slot in range(4):
                     g, half = 2 * i + slot // 2, slot % 2
                     if s >= FIRST_REORDERED:
@@ -231,10 +231,11 @@ def tile_spatialcgnl_pa_kernel(tc, x, Wt, Wp, Wg, out):
                     in_=w_grouped[r][:, g, :],
                 )
 
-        def positions_by_channels(u, m):
-            sums = bank_tile("sums%d_%d" % (u, m), next_sum_bank())
+        def positions_by_channels(u, m, passes=range(PASSES), sums=None):
+            if sums is None:
+                sums = bank_tile("sums%d_%d" % (u, m), next_sum_bank())
             cols = slice(m * P, (m + 1) * P)
-            for g in range(PASSES):
+            for g in passes:
                 nc.tensor.matmul_mx(
                     out=sums[:],
                     lhsT=x_codes[g][:, cols].bitcast(E4M3_X4),
@@ -279,8 +280,10 @@ def tile_spatialcgnl_pa_kernel(tc, x, Wt, Wp, Wg, out):
             )
 
         def t_image2_group(u, m, engine):
+            scale_image2(u, m, positions_by_channels(u, m), engine)
+
+        def scale_image2(u, m, sums, engine):
             j = units[u][1]
-            sums = positions_by_channels(u, m)
             t2_tiles[(u, m)] = t2_pool.tile([P, 512], F32, name="t2_%d_%d" % (u, m), tag="t2")
             times_att(engine, t2_tiles[(u, m)][:], sums[:], j, 2)
 
@@ -296,16 +299,19 @@ def tile_spatialcgnl_pa_kernel(tc, x, Wt, Wp, Wg, out):
                         identity[:],
                     )
                 y2 = y2_pool.tile([P, 2, 256], F32, name="y2_%d_%d" % (u, pair), tag="y2")
-                nc.vector.tensor_copy(out=y2[:].rearrange("c l n -> c (l n)"), in_=turned[:])
+                copy_on(("vector", "scalar")[pair], y2[:].rearrange("c l n -> c (l n)"), turned[:])
                 nc.sync.dma_start(
                     out=out[2, j, pair * 256 : (pair + 1) * 256, :].rearrange("(l c) n -> c l n", l=2), in_=y2[:]
                 )
 
         def t_images01_group(u, sub, engine):
-            j = units[u][1]
-            sums = bank_tile("sums01_%d_%d" % (u, sub), next_sum_bank())
+            store_images01(u, sub, channels_by_positions(u, sub), engine)
+
+        def channels_by_positions(u, sub, passes=range(PASSES), sums=None):
+            if sums is None:
+                sums = bank_tile("sums01_%d_%d" % (u, sub), next_sum_bank())
             channels = slice(sub * P, (sub + 1) * P)
-            for g in range(PASSES):
+            for g in passes:
                 nc.tensor.matmul_mx(
                     out=sums[:],
                     lhsT=w_codes[u][:, g, channels].bitcast(E5M2_X4),
@@ -315,7 +321,17 @@ def tile_spatialcgnl_pa_kernel(tc, x, Wt, Wp, Wg, out):
                     start=(g == 0),
                     stop=(g == PASSES - 1),
                 )
+            return sums
+
+        def store_images01(u, sub, sums, engine):
+            j = units[u][1]
+            channels = slice(sub * P, (sub + 1) * P)
             y01 = y01_pool.tile([P, 2, 256], F32, name="y01_%d_%d" % (u, sub), tag="y01")
+            if engine == "both":
+                for b in range(2):
+                    times_att(("scalar", "vector")[b], y01[:, b, :], sums[:, b * 256 : (b + 1) * 256], j, b)
+                    nc.sync.dma_start(out=out[b, j, channels, :], in_=y01[:, b, :])
+                return
             for b in range(2):
                 times_att(engine, y01[:, b, :], sums[:, b * 256 : (b + 1) * 256], j, b)
             nc.sync.dma_start(out=out[0:2, j, channels, :].rearrange("b c n -> c b n"), in_=y01[:])
@@ -334,21 +350,19 @@ def tile_spatialcgnl_pa_kernel(tc, x, Wt, Wp, Wg, out):
             if r in (4, 5):
                 quantise_pair(r)
 
-        for s in range(4):
-            load_strip(s)
         load_x(0)
-        for s in range(4, RAW_BUFS):
+        for s in range(RAW_BUFS):
             load_strip(s)
         load_x(1)
-        transpose_round(0)
-        transpose_round(1)
         quantise_x(0)
+        transpose_round(0)
         load_x(2)
+        transpose_round(1)
         transpose_round(2)
         transpose_round(3)
         quantise_x(1)
-        load_chunk(0)
-        load_chunk(1)
+        load_chunk(0, nc.gpsimd)
+        load_chunk(1, nc.gpsimd)
         for m in (0, 1):
             p_group(0, m)
         for m in (0, 1):
@@ -356,8 +370,8 @@ def tile_spatialcgnl_pa_kernel(tc, x, Wt, Wp, Wg, out):
         reorder_strip(FIRST_REORDERED)
         reorder_strip(FIRST_REORDERED + 1)
         quantise_x(2)
-        load_chunk(2)
-        load_chunk(3)
+        load_chunk(2, nc.gpsimd)
+        load_chunk(3, nc.gpsimd)
         for m in (2, 3):
             p_group(0, m)
         for m in (2, 3):
@@ -406,6 +420,8 @@ def tile_spatialcgnl_pa_kernel(tc, x, Wt, Wp, Wg, out):
                 g_group(u, 4)
                 quantise_pair(9)
                 g_group(u, 5)
+        sum_ring["banks"] = LATE_SUM_BANKS
+        sum_ring["next"] = 0
         for sub in (0, 1):
             t_images01_group(4, sub, "scalar")
         reorder_chunk(3)
@@ -422,7 +438,7 @@ def tile_spatialcgnl_pa_kernel(tc, x, Wt, Wp, Wg, out):
         t_image2_group(5, 5, "vector")
         t_images01_group(5, 0, "scalar")
         t_images01_group(5, 1, "vector")
+        t_images01_group(5, 2, "scalar")
         t_image2_back(4)
         t_image2_back(5)
-        t_images01_group(5, 2, "scalar")
-        t_images01_group(5, 3, "vector")
+        t_images01_group(5, 3, "both")

@@ -31,6 +31,8 @@ FIRST_REGULAR_ROUND = 6
 BLOCK_LAG = 2
 ATT_ROUND = {7: 0, 11: 1}
 RUN = 4
+EMPTIED_BY_VECTOR = ((1, 1), (3, 1), (5, 1))
+LAST_GROUP = (5, 3)
 T_UNITS = (4, 5)
 
 
@@ -207,9 +209,10 @@ def tile_spatialcgnl_pa_kernel(tc, x, Wt, Wp, Wg, out):
                 )
             words = w_grouped[pair][:].bitcast(F32).rearrange("q g (c half) -> q g c half", half=2)
             for i in range(2):
-                nc.scalar.copy(
-                    out=words[:, 2 * i : 2 * i + 2, sub * P : (sub + 1) * P, :],
-                    in_=transposed[(s, i)][:].rearrange("q (g half c) -> q g c half", g=2, half=2),
+                copy_on(
+                    "vector" if (s, i) in EMPTIED_BY_VECTOR else "scalar",
+                    words[:, 2 * i : 2 * i + 2, sub * P : (sub + 1) * P, :],
+                    transposed[(s, i)][:].rearrange("q (g half c) -> q g c half", g=2, half=2),
                 )
 
         def quantise_strip(s):
@@ -327,14 +330,27 @@ def tile_spatialcgnl_pa_kernel(tc, x, Wt, Wp, Wg, out):
             j = units[u][1]
             channels = slice(sub * P, (sub + 1) * P)
             y01 = y01_pool.tile([P, 2, 256], F32, name="y01_%d_%d" % (u, sub), tag="y01")
-            if engine == "both":
+            if (u, sub) == LAST_GROUP:
                 for b in range(2):
-                    times_att(("scalar", "vector")[b], y01[:, b, :], sums[:, b * 256 : (b + 1) * 256], j, b)
+                    times_att(engine, y01[:, b, :], sums[:, b * 256 : (b + 1) * 256], j, b)
                     nc.sync.dma_start(out=out[b, j, channels, :], in_=y01[:, b, :])
                 return
             for b in range(2):
                 times_att(engine, y01[:, b, :], sums[:, b * 256 : (b + 1) * 256], j, b)
             nc.sync.dma_start(out=out[0:2, j, channels, :].rearrange("b c n -> c b n"), in_=y01[:])
+
+        def last_unit_front():
+            u = CHUNK_UNIT
+            open_sums = {}
+            for passes in ((0,), (1,), (2,), (3,)):
+                for m in (4, 5):
+                    open_sums[m] = positions_by_channels(u, m, passes, open_sums.get(m))
+                    if passes == (3,):
+                        scale_image2(u, m, open_sums[m], "scalar" if m == 4 else "vector")
+                for sub in (0, 1):
+                    open_sums[sub] = channels_by_positions(u, sub, passes, open_sums.get(sub))
+                    if passes == (3,):
+                        store_images01(u, sub, open_sums[sub], "scalar" if sub == 0 else "vector")
 
         def transpose_round(r):
             for s in (2 * r, 2 * r + 1):
@@ -387,58 +403,52 @@ def tile_spatialcgnl_pa_kernel(tc, x, Wt, Wp, Wg, out):
             if r == 7:
                 attention(0)
             transpose_round(r)
-            h = r - BLOCK_LAG
-            u, second = h // 2, h % 2
-            first = 3 * second
+            u, second = (r - BLOCK_LAG) // 2, (r - BLOCK_LAG) % 2
             if r == 6:
                 reorder_chunk(0)
                 turn_chunk(0)
-                for m in range(first, first + 3):
+                for m in range(3):
                     p_group(u, m)
-                group_chunk(0)
                 quantise_pair(6)
                 reorder_chunk(1)
             if r == 7:
                 turn_chunk(1)
-                p_group(u, 3)
-                p_group(u, 4)
-                p_group(u, 5)
-                quantise_chunk(0)
+                for m in range(3, 6):
+                    p_group(u, m)
                 quantise_pair(7)
-                group_chunk(1)
             if r == 8:
                 g_group(u, 0)
-                reorder_chunk(2)
+                group_chunk(0)
                 g_group(u, 1)
                 quantise_pair(8)
                 g_group(u, 2)
-                quantise_chunk(1)
             if r == 9:
-                turn_chunk(2)
-                group_chunk(2)
+                group_chunk(1)
                 g_group(u, 3)
                 g_group(u, 4)
-                quantise_pair(9)
                 g_group(u, 5)
+                quantise_pair(9)
         sum_ring["banks"] = LATE_SUM_BANKS
         sum_ring["next"] = 0
+        quantise_chunk(0)
+        reorder_chunk(2)
+        turn_chunk(2)
         for sub in (0, 1):
             t_images01_group(4, sub, "scalar")
+        quantise_chunk(1)
+        group_chunk(2, "vector")
         reorder_chunk(3)
         turn_chunk(3)
-        quantise_chunk(2)
-        group_chunk(3)
+        t_images01_group(4, 2, "scalar")
         attention(1)
-        t_images01_group(4, 2, "vector")
+        quantise_chunk(2)
+        group_chunk(3, "vector")
         t_images01_group(4, 3, "scalar")
-        quantise_chunk(3)
         t_image2_group(4, 4, "scalar")
-        t_image2_group(4, 5, "vector")
-        t_image2_group(5, 4, "scalar")
-        t_image2_group(5, 5, "vector")
-        t_images01_group(5, 0, "scalar")
-        t_images01_group(5, 1, "vector")
-        t_images01_group(5, 2, "scalar")
+        quantise_chunk(3)
+        t_image2_group(4, 5, "scalar")
+        last_unit_front()
+        t_images01_group(5, 2, "vector")
         t_image2_back(4)
         t_image2_back(5)
-        t_images01_group(5, 3, "both")
+        t_images01_group(5, 3, "scalar")

@@ -71,12 +71,15 @@ def tile_spatialcgnl_pa_kernel(tc, x, Wt, Wp, Wg, out):
         x_scales = {}
         for g in range(PASSES):
             x_codes[g] = keep.tile([P, 768], U32, name="x_codes%d" % g, align_bytes=256)
-            x_scales[g] = keep.tile([P, 768], U8, name="x_scales%d" % g, align_bytes=256)
+            wide = keep.tile([P, 1024], U8, name="x_scales%d" % g, align_bytes=256)
+            x_scales[g] = wide[:, 64 : 64 + 768]
         w_codes = {}
         w_scales = {}
         for u in range(len(units)):
-            w_codes[u] = keep.tile([P, PASSES, 512], U32, name="w_codes%d" % u, align_bytes=256)
-            w_scales[u] = keep.tile([P, PASSES, 512], U8, name="w_scales%d" % u, align_bytes=256)
+            wide = keep.tile([P, 2112], U32, name="w_codes%d" % u, align_bytes=256)
+            w_codes[u] = wide[:, 32 : 32 + 2048].rearrange("q (g c) -> q g c", g=PASSES)
+            wide = keep.tile([P, 2304], U8, name="w_scales%d" % u, align_bytes=256)
+            w_scales[u] = wide[:, 192 : 192 + 2048].rearrange("q (g c) -> q g c", g=PASSES)
 
         x_raw = {}
         raw = {}
@@ -157,14 +160,14 @@ def tile_spatialcgnl_pa_kernel(tc, x, Wt, Wp, Wg, out):
             )
 
         def load_x(b):
-            for g in range(PASSES):
-                if g % 2 == 0:
-                    two_passes = x_raw_pool.tile([P, 2048], BF16, name="x_raw%d_%d" % (b, g), tag="x_raw")
-                x_raw[(b, g)] = two_passes[:, g % 2 * 1024 : (g % 2 + 1) * 1024]
+            for g in (0, 2):
+                two_passes = x_raw_pool.tile([P, 2048], BF16, name="x_raw%d_%d" % (b, g), tag="x_raw")
                 nc.sync.dma_start(
-                    out=x_raw[(b, g)],
-                    in_=x[b, g * 512 : (g + 1) * 512].rearrange("(q e) h w -> q (e h w)", e=4),
+                    out=two_passes[:].rearrange("q (f k) -> q f k", f=2),
+                    in_=x[b, g * 512 : (g + 2) * 512].rearrange("(f q e) h w -> q f (e h w)", f=2, e=4),
                 )
+                for f in (0, 1):
+                    x_raw[(b, g + f)] = two_passes[:, f * 1024 : (f + 1) * 1024]
 
         def quantise_x(b):
             grouped = {}

from contextlib import ExitStack

import concourse.masks as masks
import concourse.mybir as mybir

FLOPS = 2 * 3 * 3072 * 2048 * 256

F32 = mybir.dt.float32
BF16 = mybir.dt.bfloat16
U32 = mybir.dt.uint32
U8 = mybir.dt.uint8
E4M3_X4 = mybir.dt.float8_e4m3fn_x4
E5M2_X4 = mybir.dt.float8_e5m2_x4
COPY = mybir.ActivationFunctionType.Copy
MULT = mybir.AluOpType.mult
ADD = mybir.AluOpType.add

P = 128
PASSES = 4
STRIPS = 20
CHUNK_UNIT = 5
ROUNDS = STRIPS // 2
RAW_BUFS = 8
FIRST_REORDERED = 8
STRIPWISE_QUANTISED = 8
TRANSPOSE_BANKS = ((6, 7), (0, 1), (2, 3), (4, 5))
SUM_BANKS = (2, 3, 4, 5)
LATE_SUM_BANKS = (6, 7, 0, 1, 2, 3, 4, 5)
X_COPIES_ON_VECTOR = (3, 3, 2)
FIRST_REGULAR_ROUND = 6
BLOCK_LAG = 2
ATT_ROUND = {7: 0, 11: 1}
RUN = 4
EMPTIED_BY_VECTOR = ((1, 1), (3, 1), (5, 1))
LAST_GROUP = (5, 3)
T_UNITS = (4, 5)


def tile_spatialcgnl_pa_kernel(tc, x, Wt, Wp, Wg, out):
    nc = tc.nc
    units = [(Wp, 0), (Wg, 0), (Wp, 1), (Wg, 1), (Wt, 0), (Wt, 1)]

    with ExitStack() as ctx:
        const = ctx.enter_context(tc.tile_pool(name="const", bufs=1))
        keep = ctx.enter_context(tc.tile_pool(name="keep", bufs=1))
        raw_pool = ctx.enter_context(tc.tile_pool(name="raw", bufs=RAW_BUFS))
        reordered_pool = ctx.enter_context(tc.tile_pool(name="reordered", bufs=4))
        turned_pool = ctx.enter_context(tc.tile_pool(name="turned_chunk", bufs=2))
        x_grouped_pool = ctx.enter_context(tc.tile_pool(name="x_grouped", bufs=4))
        w_grouped_pool = ctx.enter_context(tc.tile_pool(name="w_grouped", bufs=3))
        x_raw_pool = ctx.enter_context(tc.tile_pool(name="x_raw", bufs=4))
        p_pool = ctx.enter_context(tc.tile_pool(name="p", bufs=7))
        product_pool = ctx.enter_context(tc.tile_pool(name="product", bufs=1))
        t2_pool = ctx.enter_context(tc.tile_pool(name="t2", bufs=4))
        y01_pool = ctx.enter_context(tc.tile_pool(name="y01", bufs=5))
        chunk_grouped_pool = ctx.enter_context(tc.tile_pool(name="chunk_grouped", bufs=2))
        y2_pool = ctx.enter_context(tc.tile_pool(name="y2", bufs=4))
        psum = ctx.enter_context(tc.psum_pool(name="psum", bufs=1))
        ctx.enter_context(tc.manual_schedule())

        identity = const.tile([P, P], F32, name="identity")
        masks.make_identity(nc, identity[:])
        ones = const.tile([P, P], F32, name="ones")
        nc.vector.memset(ones[:], 1.0)
        table_warm = const.tile([P, 1], F32, name="table_warm")
        nc.scalar.activation(out=table_warm[:], in_=ones[:, 0:1], func=COPY)
        pg_sums = const.tile([P, 12], F32, name="pg_sums")
        att = const.tile([P, 6], F32, name="att")

        x_codes = {}
        x_scales = {}
        for g in range(PASSES):
            x_codes[g] = keep.tile([P, 768], U32, name="x_codes%d" % g, align_bytes=256)
            wide = keep.tile([P, 1024], U8, name="x_scales%d" % g, align_bytes=256)
            x_scales[g] = wide[:, 64 : 64 + 768]
        w_codes = {}
        w_scales = {}
        for u in range(len(units)):
            wide = keep.tile([P, 2112], U32, name="w_codes%d" % u, align_bytes=256)
            w_codes[u] = wide[:, 32 : 32 + 2048].rearrange("q (g c) -> q g c", g=PASSES)
            wide = keep.tile([P, 2304], U8, name="w_scales%d" % u, align_bytes=256)
            w_scales[u] = wide[:, 192 : 192 + 2048].rearrange("q (g c) -> q g c", g=PASSES)

        x_raw = {}
        raw = {}
        reordered = {}
        chunk_raw = {}
        chunk_reordered = {}
        chunk_turned = {}
        chunk_grouped = {}
        transposed = {}
        w_grouped = {}
        p_tiles = {}
        t2_tiles = {}
        sum_ring = {"banks": SUM_BANKS, "next": 0}

        def bank_tile(name, bank):
            return psum.tile([P, 512], F32, name=name, tag="bank%d" % bank)

        def next_sum_bank():
            bank = sum_ring["banks"][sum_ring["next"] % len(sum_ring["banks"])]
            sum_ring["next"] = sum_ring["next"] + 1
            return bank

        def copy_on(engine, dst, src):
            if engine == "scalar":
                nc.scalar.copy(out=dst, in_=src)
            else:
                nc.vector.tensor_copy(out=dst, in_=src)

        def times_att(engine, dst, src, j, b):
            factor = att[:, 3 * j + b : 3 * j + b + 1]
            if engine == "scalar":
                nc.scalar.activation(out=dst, in_=src, func=COPY, scale=factor)
            else:
                nc.vector.tensor_scalar(out=dst, in0=src, scalar1=factor, scalar2=None, op0=MULT)

        def load_strip(s):
            matrix, j = units[s // 4]
            row = j * 512 + (s % 4) * P
            raw[s] = raw_pool.tile([P, 2048], BF16, name="raw%d" % s, tag="raw")
            nc.sync.dma_start(out=raw[s][:], in_=matrix[row : row + P, :])

        def load_chunk(g, queue):
            matrix, j = units[CHUNK_UNIT]
            chunk_raw[g] = x_raw_pool.tile([P, 2048], BF16, name="chunk_raw%d" % g, tag="x_raw")
            for z in range(4):
                k = slice(512 * g + 128 * z, 512 * g + 128 * (z + 1))
                queue.dma_start(
                    out=chunk_raw[g][32 * z : 32 * (z + 1), :].rearrange("r (i w) -> r i w", i=16),
                    in_=matrix[j * 512 : (j + 1) * 512, k].rearrange("(i r) w -> r i w", r=32),
                )

        def reorder_chunk(g, engine="vector"):
            chunk_reordered[g] = reordered_pool.tile([P, 1024], F32, name="chunk_reordered%d" % g, tag="reordered", align_bytes=64)
            copy_on(
                engine,
                chunk_reordered[g][:].rearrange("c (i half q) -> c i half q", i=16, half=2),
                chunk_raw[g][:].bitcast(F32).rearrange("c (i q half) -> c i half q", i=16, half=2),
            )

        def turn_chunk(g):
            chunk_turned[g] = turned_pool.tile([P, 1024], F32, name="chunk_turned%d" % g, tag="turned_chunk", align_bytes=64)
            nc.vector.transpose(out=chunk_turned[g][:], in_=chunk_reordered[g][:])

        def group_chunk(g, engine="scalar"):
            chunk_grouped[g] = chunk_grouped_pool.tile(
                [P, 2048], BF16, name="chunk_grouped%d" % g, tag="chunk_grouped", align_bytes=64
            )
            copy_on(
                engine,
                chunk_grouped[g][:].bitcast(F32).rearrange("q (i r half) -> q i r half", i=16, half=2),
                chunk_turned[g][:].rearrange("q (i half r) -> q i r half", i=16, half=2),
            )

        def quantise_chunk(g):
            u = CHUNK_UNIT
            nc.vector.quantize_mx(
                out=w_codes[u][:, g, :].bitcast(E5M2_X4), scales=w_scales[u][:, g, :], in_=chunk_grouped[g][:]
            )

        def load_x(b):
            for g in (0, 2):
                two_passes = x_raw_pool.tile([P, 2048], BF16, name="x_raw%d_%d" % (b, g), tag="x_raw")
                nc.sync.dma_start(
                    out=two_passes[:].rearrange("q (f k) -> q f k", f=2),
                    in_=x[b, g * 512 : (g + 2) * 512].rearrange("(f q e) h w -> q f (e h w)", f=2, e=4),
                )
                for f in (0, 1):
                    x_raw[(b, g + f)] = two_passes[:, f * 1024 : (f + 1) * 1024]

        def quantise_x(b):
            grouped = {}
            for g in range(PASSES):
                grouped[g] = x_grouped_pool.tile(
                    [P, 1024], BF16, name="x_grouped%d_%d" % (b, g), tag="x_grouped", align_bytes=64
                )
                copy_on(
                    "vector" if g < X_COPIES_ON_VECTOR[b] else "scalar",
                    grouped[g][:].rearrange("q (c i e) -> q c e i", i=RUN, e=4),
                    x_raw[(b, g)].rearrange("q (e c i) -> q c e i", i=RUN, e=4),
                )
            for g in range(PASSES):
                cols = slice(b * 256, (b + 1) * 256)
                nc.vector.quantize_mx(
                    out=x_codes[g][:, cols].bitcast(E4M3_X4), scales=x_scales[g][:, cols], in_=grouped[g][:]
                )

        def reorder_strip(s):
            reordered[s] = reordered_pool.tile([P, 1024], F32, name="reordered%d" % s, tag="reordered", align_bytes=64)
            nc.vector.tensor_copy(
                out=reordered[s][:].rearrange("c (g half q) -> c g half q", g=PASSES, half=2),
                in_=raw[s][:].bitcast(F32).rearrange("c (g q half) -> c g half q", g=PASSES, half=2),
            )

        def transpose_strip(s):
            for i in range(2):
                transposed[(s, i)] = bank_tile("transposed%d_%d" % (s, i), TRANSPOSE_BANKS[s % (4 if s < STRIPWISE_QUANTISED else 2)][i])
                for slot in range(4):
                    g, half = 2 * i + slot // 2, slot % 2
                    if s >= FIRST_REORDERED:
                        block = reordered[s][:, (2 * g + half) * P : (2 * g + half + 1) * P]
                    else:
                        block = raw[s][:].bitcast(F32)[:, 256 * g + half : 256 * (g + 1) : 2]
                    nc.tensor.transpose(transposed[(s, i)][:, slot * P : (slot + 1) * P], block, identity[:])

        def empty_transposes(s):
            pair, sub = s // 2, s % 2
            if sub == 0:
                w_grouped[pair] = w_grouped_pool.tile(
                    [P, PASSES, 1024], BF16, name="w_grouped%d" % pair, tag="w_grouped", align_bytes=64
                )
            words = w_grouped[pair][:].bitcast(F32).rearrange("q g (c half) -> q g c half", half=2)
            for i in range(2):
                copy_on(
                    "vector" if (s, i) in EMPTIED_BY_VECTOR else "scalar",
                    words[:, 2 * i : 2 * i + 2, sub * P : (sub + 1) * P, :],
                    transposed[(s, i)][:].rearrange("q (g half c) -> q g c half", g=2, half=2),
                )

        def quantise_strip(s):
            u, sub = s // 4, s % 4
            channels = slice(sub * P, (sub + 1) * P)
            for g in range(PASSES):
                nc.vector.quantize_mx(
                    out=w_codes[u][:, g, channels].bitcast(E5M2_X4),
                    scales=w_scales[u][:, g, channels],
                    in_=w_grouped[s // 2][:, g, s % 2 * 512 : (s % 2 + 1) * 512],
                )

        def quantise_pair(r):
            u = r // 2
            channels = slice((r % 2) * 256, (r % 2 + 1) * 256)
            for g in range(PASSES):
                nc.vector.quantize_mx(
                    out=w_codes[u][:, g, channels].bitcast(E5M2_X4), scales=w_scales[u][:, g, channels],
                    in_=w_grouped[r][:, g, :],
                )

        def positions_by_channels(u, m, passes=range(PASSES), sums=None):
            if sums is None:
                sums = bank_tile("sums%d_%d" % (u, m), next_sum_bank())
            cols = slice(m * P, (m + 1) * P)
            for g in passes:
                nc.tensor.matmul_mx(
                    out=sums[:],
                    lhsT=x_codes[g][:, cols].bitcast(E4M3_X4),
                    lhsT_scale=x_scales[g][:, cols],
                    rhs=w_codes[u][:, g, :].bitcast(E5M2_X4),
                    rhs_scale=w_scales[u][:, g, :],
                    start=(g == 0),
                    stop=(g == PASSES - 1),
                )
            return sums

        def p_group(u, m):
            j = units[u][1]
            sums = positions_by_channels(u, m)
            p_tiles[(j, m)] = p_pool.tile([P, 512], F32, name="p%d_%d" % (j, m), tag="p")
            nc.scalar.copy(out=p_tiles[(j, m)][:], in_=sums[:])

        def g_group(u, m):
            j = units[u][1]
            sums = positions_by_channels(u, m)
            product = product_pool.tile([P, 512], F32, name="product%d_%d" % (j, m), tag="product")
            nc.vector.scalar_tensor_tensor(
                out=product[:],
                in0=sums[:],
                scalar=1.0,
                in1=p_tiles[(j, m)][:],
                op0=MULT,
                op1=MULT,
                accum_out=pg_sums[:, 6 * j + m : 6 * j + m + 1],
            )

        def attention(j):
            totals = bank_tile("totals%d" % j, next_sum_bank())
            nc.tensor.matmul(
                out=totals[:, 0:6], lhsT=ones[:], rhs=pg_sums[:, 6 * j : 6 * j + 6], start=True, stop=True
            )
            nc.vector.tensor_reduce(
                out=att[:, 3 * j : 3 * j + 3],
                in_=totals[:, 0:6].rearrange("q (b h) -> q b h", h=2),
                axis=mybir.AxisListType.X,
                op=ADD,
            )

        def t_image2_group(u, m, engine):
            scale_image2(u, m, positions_by_channels(u, m), engine)

        def scale_image2(u, m, sums, engine):
            j = units[u][1]
            t2_tiles[(u, m)] = t2_pool.tile([P, 512], F32, name="t2_%d_%d" % (u, m), tag="t2")
            times_att(engine, t2_tiles[(u, m)][:], sums[:], j, 2)

        def t_image2_back(u):
            j = units[u][1]
            for pair in range(2):
                turned = bank_tile("turned%d_%d" % (u, pair), next_sum_bank())
                for slot in range(4):
                    sub, h = 2 * pair + slot // 2, slot % 2
                    nc.tensor.transpose(
                        turned[:, slot * P : (slot + 1) * P],
                        t2_tiles[(u, 4 + h)][:, sub * P : (sub + 1) * P],
                        identity[:],
                    )
                y2 = y2_pool.tile([P, 2, 256], F32, name="y2_%d_%d" % (u, pair), tag="y2")
                copy_on(("vector", "scalar")[pair], y2[:].rearrange("c l n -> c (l n)"), turned[:])
                nc.sync.dma_start(
                    out=out[2, j, pair * 256 : (pair + 1) * 256, :].rearrange("(l c) n -> c l n", l=2), in_=y2[:]
                )

        def t_images01_group(u, sub, engine):
            store_images01(u, sub, channels_by_positions(u, sub), engine)

        def channels_by_positions(u, sub, passes=range(PASSES), sums=None):
            if sums is None:
                sums = bank_tile("sums01_%d_%d" % (u, sub), next_sum_bank())
            channels = slice(sub * P, (sub + 1) * P)
            for g in passes:
                nc.tensor.matmul_mx(
                    out=sums[:],
                    lhsT=w_codes[u][:, g, channels].bitcast(E5M2_X4),
                    lhsT_scale=w_scales[u][:, g, channels],
                    rhs=x_codes[g][:, 0:512].bitcast(E4M3_X4),
                    rhs_scale=x_scales[g][:, 0:512],
                    start=(g == 0),
                    stop=(g == PASSES - 1),
                )
            return sums

        def store_images01(u, sub, sums, engine):
            j = units[u][1]
            channels = slice(sub * P, (sub + 1) * P)
            y01 = y01_pool.tile([P, 2, 256], F32, name="y01_%d_%d" % (u, sub), tag="y01")
            if (u, sub) == LAST_GROUP:
                for b in range(2):
                    times_att(engine, y01[:, b, :], sums[:, b * 256 : (b + 1) * 256], j, b)
                    nc.sync.dma_start(out=out[b, j, channels, :], in_=y01[:, b, :])
                return
            for b in range(2):
                times_att(engine, y01[:, b, :], sums[:, b * 256 : (b + 1) * 256], j, b)
            nc.sync.dma_start(out=out[0:2, j, channels, :].rearrange("b c n -> c b n"), in_=y01[:])

        def last_unit_front():
            u = CHUNK_UNIT
            open_sums = {}
            for passes in ((0,), (1,), (2,), (3,)):
                for m in (4, 5):
                    open_sums[m] = positions_by_channels(u, m, passes, open_sums.get(m))
                    if passes == (3,):
                        scale_image2(u, m, open_sums[m], "scalar" if m == 4 else "vector")
                for sub in (0, 1):
                    open_sums[sub] = channels_by_positions(u, sub, passes, open_sums.get(sub))
                    if passes == (3,):
                        store_images01(u, sub, open_sums[sub], "scalar" if sub == 0 else "vector")

        def transpose_round(r):
            for s in (2 * r, 2 * r + 1):
                transpose_strip(s)
                empty_transposes(s)
                if s + RAW_BUFS < STRIPS:
                    load_strip(s + RAW_BUFS)
                if s < STRIPWISE_QUANTISED:
                    quantise_strip(s)
            for s in (2 * r + 2, 2 * r + 3):
                if FIRST_REORDERED + 2 <= s < STRIPS:
                    reorder_strip(s)
            if r in (4, 5):
                quantise_pair(r)

        load_x(0)
        for s in range(RAW_BUFS):
            load_strip(s)
        load_x(1)
        quantise_x(0)
        transpose_round(0)
        load_x(2)
        transpose_round(1)
        transpose_round(2)
        transpose_round(3)
        quantise_x(1)
        load_chunk(0, nc.gpsimd)
        load_chunk(1, nc.gpsimd)
        for m in (0, 1):
            p_group(0, m)
        for m in (0, 1):
            g_group(1, m)
        reorder_strip(FIRST_REORDERED)
        reorder_strip(FIRST_REORDERED + 1)
        quantise_x(2)
        load_chunk(2, nc.gpsimd)
        load_chunk(3, nc.gpsimd)
        for m in (2, 3):
            p_group(0, m)
        for m in (2, 3):
            g_group(1, m)
        transpose_round(4)
        for m in (4, 5):
            p_group(0, m)
        transpose_round(5)
        for m in (4, 5):
            g_group(1, m)

        for r in range(FIRST_REGULAR_ROUND, ROUNDS):
            if r == 7:
                attention(0)
            transpose_round(r)
            u, second = (r - BLOCK_LAG) // 2, (r - BLOCK_LAG) % 2
            if r == 6:
                reorder_chunk(0)
                turn_chunk(0)
                for m in range(3):
                    p_group(u, m)
                quantise_pair(6)
                reorder_chunk(1)
            if r == 7:
                turn_chunk(1)
                for m in range(3, 6):
                    p_group(u, m)
                quantise_pair(7)
            if r == 8:
                g_group(u, 0)
                group_chunk(0)
                g_group(u, 1)
                quantise_pair(8)
                g_group(u, 2)
            if r == 9:
                group_chunk(1)
                g_group(u, 3)
                g_group(u, 4)
                g_group(u, 5)
                quantise_pair(9)
        sum_ring["banks"] = LATE_SUM_BANKS
        sum_ring["next"] = 0
        quantise_chunk(0)
        reorder_chunk(2)
        turn_chunk(2)
        for sub in (0, 1):
            t_images01_group(4, sub, "scalar")
        quantise_chunk(1)
        group_chunk(2, "vector")
        reorder_chunk(3)
        turn_chunk(3)
        t_images01_group(4, 2, "scalar")
        attention(1)
        quantise_chunk(2)
        group_chunk(3, "vector")
        t_images01_group(4, 3, "scalar")
        t_image2_group(4, 4, "scalar")
        quantise_chunk(3)
        t_image2_group(4, 5, "scalar")
        last_unit_front()
        t_images01_group(5, 2, "vector")
        t_image2_back(4)
        t_image2_back(5)
        t_images01_group(5, 3, "scalar")
